import numpy as np
import ml_dtypes


def mxq(x, axis, fmt="e4m3"):
    dtype, down = {"e4m3": (ml_dtypes.float8_e4m3fn, 7), "e5m2": (ml_dtypes.float8_e5m2, 14)}[fmt]
    v = np.moveaxis(np.asarray(x, np.float32).astype(ml_dtypes.bfloat16).astype(np.float64), axis, -1)
    blocks = v.reshape(v.shape[:-1] + (-1, 32))
    amax = np.abs(blocks).max(-1, keepdims=True)
    byte = np.maximum(np.where(amax > 0, np.frexp(amax)[1] - 1 + 127, 0) - down, 1)
    scale = np.exp2(byte - 127.0)
    codes = (blocks / scale).astype(np.float32).astype(dtype).astype(np.float64)
    return np.moveaxis((codes * scale).reshape(v.shape), -1, axis)


WIDE = False


def mx_kscale(k):
    if not WIDE:
        return np.ones(k)
    levels = np.array([10, -10, 5, -5, 0])
    a = np.random.permutation(np.resize(levels, k // 512 * 4)).reshape(k // 512, 4)
    idx = np.arange(k)
    return np.exp2(a[idx // 512, idx % 128 // 32])


BF16 = ml_dtypes.bfloat16


def bf(x):
    return np.asarray(x, np.float32).astype(BF16)


def f64(x):
    return np.asarray(x).astype(np.float64)


B, V, H = 4096, 128, 512
G = 4 * H
EPS = 1e-5


def sigmoid(v):
    return 1.0 / (1.0 + np.exp(-v))


def layer_norm(v, w, b):
    mu = v.mean(-1, keepdims=True)
    var = ((v - mu) ** 2).mean(-1, keepdims=True)
    return (v - mu) / np.sqrt(var + EPS) * w + b


def setup_inputs():
    s = mx_kscale(H)
    return {"x": bf(np.random.standard_normal((B, V))),
            "h0": bf(np.random.standard_normal((B, H)) * s),
            "c0": bf(np.random.standard_normal((B, H))),
            "w_ih1": bf(np.random.standard_normal((G, V)) / np.sqrt(V)),
            "w_hh1": bf(np.random.standard_normal((G, H)) / np.sqrt(H) / s),
            "lni_w1": bf(1.0 + 0.1 * np.random.standard_normal(G)),
            "lni_b1": bf(0.1 * np.random.standard_normal(G)),
            "lnh_w1": bf(1.0 + 0.1 * np.random.standard_normal(G)),
            "lnh_b1": bf(0.1 * np.random.standard_normal(G)),
            "lnc_w1": bf(1.0 + 0.1 * np.random.standard_normal(H)),
            "lnc_b1": bf(0.1 * np.random.standard_normal(H))}


def reference(x, h0, c0, w_ih1, w_hh1, lni_w1, lni_b1, lnh_w1, lnh_b1, lnc_w1, lnc_b1):
    a = f64(x) @ f64(w_ih1).T
    r = mxq(f64(h0), 1, "e4m3") @ mxq(f64(w_hh1), 1, "e4m3").T
    gates = layer_norm(a, f64(lni_w1), f64(lni_b1)) + layer_norm(r, f64(lnh_w1), f64(lnh_b1))
    i, f, g, o = np.split(gates, 4, axis=1)
    cy = layer_norm(sigmoid(f) * f64(c0) + sigmoid(i) * np.tanh(g), f64(lnc_w1), f64(lnc_b1))
    hy = sigmoid(o) * np.tanh(cy)
    return hy, cy

@@ -1,0 +1,330 @@
+from contextlib import ExitStack
+
+import concourse.mybir as mybir
+from concourse.masks import make_identity
+
+F32 = mybir.dt.float32
+BF16 = mybir.dt.bfloat16
+U32 = mybir.dt.uint32
+U8 = mybir.dt.uint8
+FP8X4 = mybir.dt.float8_e4m3fn_x4
+ALU = mybir.AluOpType
+ACT = mybir.ActivationFunctionType
+AX = mybir.AxisListType
+
+P = 128
+B, V, H = 4096, 128, 512
+G = 4 * H
+NT = B // P
+ST = 4
+EPS = 1e-5
+FLOPS = 2 * B * G * (H + V)
+
+
+def tile_multilstm_pa_t_kernel(
+    tc, x, h0, c0, w_ih1, w_hh1, lni_w1, lni_b1, lnh_w1, lnh_b1, lnc_w1, lnc_b1, out_0, out_1
+):
+    nc = tc.nc
+    x_v = x.rearrange("(p t) v -> p t v", t=NT)
+    h0_v = h0.rearrange("(p t) k -> p t k", t=NT)
+    c0_v = c0.rearrange("(p t) k -> p t k", t=NT)
+    hy_v = out_0.rearrange("(p t) k -> p t k", t=NT)
+    cy_v = out_1.rearrange("(p t) k -> p t k", t=NT)
+    whh_v = w_hh1.rearrange("(t p) k -> p t k", p=P)
+    wih_v = w_ih1.rearrange("(t p) v -> p t v", p=P)
+
+    with ExitStack() as ctx:
+        const = ctx.enter_context(tc.tile_pool(name="const", bufs=1))
+        small = ctx.enter_context(tc.tile_pool(name="small", bufs=4))
+        gates = ctx.enter_context(tc.tile_pool(name="gates", bufs=10))
+        ps_r = ctx.enter_context(tc.psum_pool(name="ps_r", bufs=4))
+        ps_a = ctx.enter_context(tc.psum_pool(name="ps_a", bufs=4))
+
+        ident_f = const.tile([P, P], F32, name="ident_f")
+        make_identity(nc, ident_f[:])
+        ident_b = const.tile([P, P], BF16, name="ident_b")
+        make_identity(nc, ident_b[:])
+        mhalf = const.tile([P, NT], F32, name="mhalf")
+        nc.vector.memset(mhalf[:], -0.5)
+        ones_b = const.tile([P, 2], BF16, name="ones_b")
+        nc.vector.memset(ones_b[:], 1.0)
+
+        w_codes = const.tile([P, G], U32, name="w_codes", align_bytes=64)
+        w_scales = const.tile([P, G], U8, name="w_scales", align_bytes=64)
+        h_codes = const.tile([P, B], U32, name="h_codes", align_bytes=64)
+        h_scales = const.tile([P, B], U8, name="h_scales", align_bytes=64)
+        x_t = const.tile([P, B], BF16, name="x_t")
+        w_t = const.tile([P, G], BF16, name="w_t")
+        wh_bc = const.tile([P, G], BF16, name="wh_bc")
+        cw_bc = const.tile([P, H], BF16, name="cw_bc")
+        cb_bc = const.tile([P, H], BF16, name="cb_bc")
+        g_hl = const.tile([P, 2, P], BF16, name="g_hl")
+        ws_hl = const.tile([P, 2, 2], BF16, name="ws_hl")
+        v_t = const.tile([P, 48], F32, name="v_t")
+        b_t = const.tile([P, 16], F32, name="b_t")
+        sum_a = const.tile([P, NT], F32, name="sum_a")
+        sumsq_a = const.tile([P, NT], F32, name="sumsq_a")
+        mu_a = const.tile([P, NT], F32, name="mu_a")
+        musq_a = const.tile([P, NT], F32, name="musq_a")
+        var_a = const.tile([P, NT], F32, name="var_a")
+        ve_a = const.tile([P, NT], F32, name="ve_a")
+        rs_a = const.tile([P, NT], F32, name="rs_a")
+        nb_a = const.tile([P, NT], F32, name="nb_a")
+
+        with tc.tile_pool(name="pro", bufs=1) as pro, tc.tile_pool(name="stage", bufs=3) as stg:
+            x_sb = pro.tile([P, NT, V], BF16, name="x_sb")
+            w_n = pro.tile([P, 16, V], BF16, name="w_n")
+            vec = pro.tile([P, P], BF16, name="vec")
+            nc.vector.memset(vec[:], 0.0)
+            nc.scalar.dma_start(out=w_n[:], in_=wih_v)
+            nc.scalar.dma_start(out=x_sb[:], in_=x_v)
+            nc.scalar.dma_start(out=vec[0:16, :], in_=lni_w1.rearrange("(t p) -> t p", p=P))
+            nc.scalar.dma_start(out=vec[16:32, :], in_=lni_b1.rearrange("(t p) -> t p", p=P))
+            nc.scalar.dma_start(out=vec[32:48, :], in_=lnh_b1.rearrange("(t p) -> t p", p=P))
+            nc.scalar.dma_start(out=wh_bc[:], in_=lnh_w1.partition_broadcast(P))
+            nc.scalar.dma_start(out=cw_bc[:], in_=lnc_w1.partition_broadcast(P))
+            nc.scalar.dma_start(out=cb_bc[:], in_=lnc_b1.partition_broadcast(P))
+
+            def pack_rows(src, codes, scales):
+                raw = stg.tile([P, ST * H], BF16, name="raw", tag="raw")
+                nc.sync.dma_start(out=raw[:].rearrange("p (t k) -> p t k", t=ST), in_=src)
+                words = raw[:].bitcast(F32)
+                grouped = stg.tile([P, ST * P * 4], BF16, name="grouped", tag="grouped", align_bytes=64)
+                g_words = grouped[:].bitcast(F32).rearrange("p (t c u) -> p t c u", t=ST, u=2)
+                for half in range(2):
+                    bank = ps_a.tile([P, 2, 2, P], F32, name="tp_w", tag="ap")
+                    for i in range(2):
+                        for u in range(2):
+                            col = (2 * half + i) * (H // 2) + u * P
+                            nc.tensor.transpose(bank[:, i, u, :], words[:, col:col + P], ident_f[:])
+                    src_v = bank[:].rearrange("p t u c -> p t c u")
+                    dst_v = g_words[:, 2 * half:2 * half + 2, :, :]
+                    if half == 0:
+                        nc.vector.tensor_copy(out=dst_v, in_=src_v)
+                    else:
+                        nc.scalar.copy(out=dst_v, in_=src_v)
+                nc.vector.quantize_mx(out=codes.bitcast(FP8X4), scales=scales, in_=grouped[:])
+
+            for g in range(4):
+                cols = slice(g * H, (g + 1) * H)
+                pack_rows(whh_v[:, ST * g:ST * (g + 1), :], w_codes[:, cols], w_scales[:, cols])
+            for s in range(NT // ST):
+                cols = slice(s * H, (s + 1) * H)
+                pack_rows(h0_v[:, ST * s:ST * (s + 1), :], h_codes[:, cols], h_scales[:, cols])
+
+            bank = ps_a.tile([P, P], BF16, name="tp_v", tag="ap")
+            nc.tensor.transpose(bank[:], vec[:], ident_b[:])
+            nc.vector.tensor_copy(out=v_t[:], in_=bank[:, 0:48])
+            nc.vector.tensor_tensor(out=b_t[:], in0=v_t[:, 16:32], in1=v_t[:, 32:48], op=ALU.add)
+
+            for g in range(4):
+                bank = ps_a.tile([P, 4, P], BF16, name="tp_b", tag="ap")
+                for i in range(4):
+                    nc.tensor.transpose(bank[:, i, :], w_n[:, 4 * g + i, :], ident_b[:])
+                nc.scalar.copy(out=w_t[:, 4 * g * P:4 * (g + 1) * P], in_=bank[:].rearrange("p t c -> p (t c)"))
+            for g in range(NT // 4):
+                bank = ps_a.tile([P, 4, P], BF16, name="tp_b", tag="ap")
+                for i in range(4):
+                    nc.tensor.transpose(bank[:, i, :], x_sb[:, 4 * g + i, :], ident_b[:])
+                nc.scalar.copy(out=x_t[:, 4 * g * P:4 * (g + 1) * P], in_=bank[:].rearrange("p t c -> p (t c)"))
+
+            g_ps = ps_a.tile([P, P + 2], F32, name="g_ps", tag="ap")
+            for t in range(16):
+                nc.tensor.matmul(g_ps[:, 0:P], lhsT=w_n[:, t, :], rhs=w_n[:, t, :], start=(t == 0), stop=(t == 15))
+            for t in range(16):
+                nc.tensor.matmul(g_ps[:, P:P + 2], lhsT=w_n[:, t, :], rhs=ones_b[:], start=(t == 0), stop=(t == 15))
+            nc.vector.tensor_copy(out=g_hl[:, 0, :], in_=g_ps[:, 0:P])
+            nc.vector.tensor_tensor(out=g_hl[:, 1, :], in0=g_ps[:, 0:P], in1=g_hl[:, 0, :], op=ALU.subtract)
+            nc.vector.tensor_copy(out=ws_hl[:, 0, :], in_=g_ps[:, P:P + 2])
+            nc.vector.tensor_tensor(out=ws_hl[:, 1, :], in0=g_ps[:, P:P + 2], in1=ws_hl[:, 0, :], op=ALU.subtract)
+
+            m_ps = ps_r.tile([P, NT, 4], F32, name="m_ps", tag="r")
+            for g in range(NT // 2):
+                y_ps = ps_a.tile([P, 2, 2, P], F32, name="y_ps", tag="ap")
+                for i in range(2):
+                    t = 2 * g + i
+                    lhs = x_t[:, t * P:(t + 1) * P]
+                    nc.tensor.matmul(
+                        y_ps[:, i, :, :].rearrange("p h v -> p (h v)"),
+                        lhsT=lhs,
+                        rhs=g_hl[:].rearrange("p h v -> p (h v)"),
+                        start=True,
+                        stop=True,
+                    )
+                    nc.tensor.matmul(
+                        m_ps[:, t, :], lhsT=lhs, rhs=ws_hl[:].rearrange("p h n -> p (h n)"), start=True, stop=True
+                    )
+                for i in range(2):
+                    t = 2 * g + i
+                    junk = pro.tile([P, 2, P], F32, name="junk", tag="junk", bufs=2)
+                    nc.vector.scalar_tensor_tensor(
+                        out=junk[:],
+                        in0=y_ps[:, i, :, :],
+                        scalar=1.0,
+                        in1=x_sb[:, t, :].unsqueeze(1).to_broadcast([P, 2, P]),
+                        op0=ALU.mult,
+                        op1=ALU.mult,
+                        accum_out=sumsq_a[:, t:t + 1],
+                    )
+            nc.vector.tensor_reduce(out=sum_a[:], in_=m_ps[:], axis=AX.X, op=ALU.add)
+            nc.vector.tensor_scalar(out=mu_a[:], in0=sum_a[:], scalar1=1.0 / (2 * G), scalar2=None, op0=ALU.mult)
+            nc.vector.tensor_tensor(out=musq_a[:], in0=mu_a[:], in1=mu_a[:], op=ALU.mult)
+            nc.vector.scalar_tensor_tensor(
+                out=var_a[:], in0=sumsq_a[:], scalar=1.0 / G, in1=musq_a[:], op0=ALU.mult, op1=ALU.subtract
+            )
+            nc.vector.tensor_scalar(out=ve_a[:], in0=var_a[:], scalar1=0.0, scalar2=EPS, op0=ALU.max, op1=ALU.add)
+            nc.gpsimd.tensor_tensor(out=rs_a[:], in0=ve_a[:], in1=mhalf[:], op=ALU.pow)
+            nc.vector.scalar_tensor_tensor(
+                out=nb_a[:], in0=mu_a[:], scalar=-1.0, in1=rs_a[:], op0=ALU.mult, op1=ALU.mult
+            )
+
+        work = ctx.enter_context(tc.tile_pool(name="work", bufs=2))
+
+        gt = {}
+        rs_r = {}
+        ahat = {}
+        p2t = {}
+        c0s = {}
+
+        def r_phase(t):
+            banks = []
+            rows = slice(t * P, (t + 1) * P)
+            for c in range(4):
+                bank = ps_r.tile([P, H], F32, name="r_ps", tag="r")
+                cols = slice(c * H, (c + 1) * H)
+                nc.tensor.matmul_mx(
+                    out=bank[:],
+                    lhsT=h_codes[:, rows].bitcast(FP8X4),
+                    lhsT_scale=h_scales[:, rows],
+                    rhs=w_codes[:, cols].bitcast(FP8X4),
+                    rhs_scale=w_scales[:, cols],
+                    start=True,
+                    stop=True,
+                )
+                banks.append(bank)
+            st = small.tile([P, 4, 6], F32, name="st_r", tag="st_r")
+            for c in range(4):
+                nc.vector.bn_stats(out=st[:, c, :], in_=banks[c][:])
+            mv = small.tile([P, 2], F32, name="mv_r", tag="mv_r")
+            nc.vector.bn_aggr(out=mv[:], in_=st[:].rearrange("p c s -> p (c s)"))
+            ve = small.tile([P, 1], F32, name="ve_r", tag="ve_r")
+            nc.vector.tensor_scalar(out=ve[:], in0=mv[:, 1:2], scalar1=EPS, scalar2=None, op0=ALU.add)
+            rs = small.tile([P, 1], F32, name="rs_r", tag="rs_r", bufs=12)
+            nc.gpsimd.tensor_tensor(out=rs[:], in0=ve[:], in1=mhalf[:, 0:1], op=ALU.pow)
+            rs_r[t] = rs
+            gate = gates.tile([P, G], F32, name="gate", tag="gate")
+            for c in range(4):
+                cols = slice(c * H, (c + 1) * H)
+                nc.vector.scalar_tensor_tensor(
+                    out=gate[:, cols],
+                    in0=banks[c][:],
+                    scalar=mv[:, 0:1],
+                    in1=wh_bc[:, cols],
+                    op0=ALU.subtract,
+                    op1=ALU.mult,
+                )
+            gt[t] = gate
+
+        def a1(k):
+            s, c = divmod(k, 4)
+            if c == 0:
+                c0_sb = work.tile([P, ST, H], BF16, name="c0_sb", tag="c0_sb", bufs=3)
+                nc.sync.dma_start(out=c0_sb[:], in_=c0_v[:, ST * s:ST * (s + 1), :])
+                c0s[s] = c0_sb
+            ah = work.tile([P, ST, H], F32, name="ahat", tag="ahat")
+            for bt in range(ST):
+                t = ST * s + bt
+                bank = ps_a.tile([P, H], F32, name="a_ps", tag="ap")
+                nc.tensor.matmul(
+                    bank[:], lhsT=x_t[:, t * P:(t + 1) * P], rhs=w_t[:, c * H:(c + 1) * H], start=True, stop=True
+                )
+                nc.scalar.activation(
+                    out=ah[:, bt, :], in_=bank[:], func=ACT.Identity, bias=nb_a[:, t:t + 1], scale=rs_a[:, t:t + 1]
+                )
+            ahat[k] = ah
+
+        def a2(k):
+            c = k % 4
+            ah = ahat[k]
+            pt = work.tile([P, 4, ST * P], F32, name="p2t", tag="p2t")
+            for jb in range(4):
+                bank = ps_a.tile([P, ST, P], F32, name="t_ps", tag="ap")
+                for bt in range(ST):
+                    nc.tensor.transpose(bank[:, bt, :], ah[:, bt, jb * P:(jb + 1) * P], ident_f[:])
+                col = 4 * c + jb
+                nc.scalar.activation(
+                    out=pt[:, jb, :],
+                    in_=bank[:].rearrange("p t b -> p (t b)"),
+                    func=ACT.Identity,
+                    bias=b_t[:, col:col + 1],
+                    scale=v_t[:, col:col + 1],
+                )
+            p2t[k] = pt
+
+        def a3(k):
+            s, c = divmod(k, 4)
+            pt = p2t[k]
+            for bt in range(ST):
+                t = ST * s + bt
+                bank = ps_a.tile([P, 4, P], F32, name="p_ps", tag="ap")
+                for jb in range(4):
+                    nc.tensor.transpose(bank[:, jb, :], pt[:, jb, bt * P:(bt + 1) * P], ident_f[:])
+                dst = gt[t][:, c * H:(c + 1) * H]
+                nc.vector.scalar_tensor_tensor(
+                    out=dst,
+                    in0=dst,
+                    scalar=rs_r[t][:, 0:1],
+                    in1=bank[:].rearrange("p j c -> p (j c)"),
+                    op0=ALU.mult,
+                    op1=ALU.add,
+                )
+
+        def a4(k):
+            s, c = divmod(k, 4)
+            for bt in range(ST):
+                dst = gt[ST * s + bt][:, c * H:(c + 1) * H]
+                nc.scalar.activation(out=dst, in_=dst, func=(ACT.Tanh if c == 2 else ACT.Sigmoid))
+
+        def cell(t):
+            s, bt = divmod(t, ST)
+            gate = gt[t]
+            c1 = work.tile([P, H], F32, name="c1", tag="c1")
+            c2 = work.tile([P, H], F32, name="c2", tag="c2")
+            nc.gpsimd.tensor_tensor(out=c1[:], in0=gate[:, H:2 * H], in1=c0s[s][:, bt, :], op=ALU.mult)
+            nc.gpsimd.tensor_tensor(out=c2[:], in0=gate[:, 0:H], in1=gate[:, 2 * H:3 * H], op=ALU.mult)
+            nc.gpsimd.tensor_tensor(out=c1[:], in0=c1[:], in1=c2[:], op=ALU.add)
+            st = small.tile([P, 6], F32, name="st_c", tag="st_c")
+            nc.vector.bn_stats(out=st[:], in_=c1[:])
+            mv = small.tile([P, 2], F32, name="mv_c", tag="mv_c")
+            nc.vector.bn_aggr(out=mv[:], in_=st[:])
+            ve = small.tile([P, 1], F32, name="ve_c", tag="ve_c")
+            nc.vector.tensor_scalar(out=ve[:], in0=mv[:, 1:2], scalar1=EPS, scalar2=None, op0=ALU.add)
+            rs = small.tile([P, 1], F32, name="rs_c", tag="rs_c")
+            nc.gpsimd.tensor_tensor(out=rs[:], in0=ve[:], in1=mhalf[:, 0:1], op=ALU.pow)
+            nc.vector.scalar_tensor_tensor(
+                out=c2[:], in0=c1[:], scalar=mv[:, 0:1], in1=cw_bc[:], op0=ALU.subtract, op1=ALU.mult
+            )
+            cy = work.tile([P, H], F32, name="cy", tag="cy", bufs=3)
+            nc.vector.scalar_tensor_tensor(
+                out=cy[:], in0=c2[:], scalar=rs[:, 0:1], in1=cb_bc[:], op0=ALU.mult, op1=ALU.add
+            )
+            nc.sync.dma_start(out=cy_v[:, t, :], in_=cy[:])
+            tcy = work.tile([P, H], F32, name="tcy", tag="tcy")
+            nc.scalar.activation(out=tcy[:], in_=cy[:], func=ACT.Tanh)
+            hy = work.tile([P, H], F32, name="hy", tag="hy", bufs=3)
+            nc.gpsimd.tensor_tensor(out=hy[:], in0=gate[:, 3 * H:4 * H], in1=tcy[:], op=ALU.mult)
+            nc.sync.dma_start(out=hy_v[:, t, :], in_=hy[:])
+
+        for n in range(-4, NT + 5):
+            if 0 <= n - 5 < NT:
+                cell(n - 5)
+            if 0 <= n - 1 < NT:
+                a4(n - 1)
+            if 0 <= n < NT:
+                a3(n)
+            if 0 <= n + 1 < NT:
+                a2(n + 1)
+            if 0 <= n + 2 < NT:
+                a1(n + 2)
+            if 0 <= n + 4 < NT:
+                r_phase(n + 4)

@@ -35,10 +35,9 @@ def tile_multilstm_pa_t_kernel(
 
     with ExitStack() as ctx:
         const = ctx.enter_context(tc.tile_pool(name="const", bufs=1))
-        small = ctx.enter_context(tc.tile_pool(name="small", bufs=4))
-        gates = ctx.enter_context(tc.tile_pool(name="gates", bufs=10))
-        ps_r = ctx.enter_context(tc.psum_pool(name="ps_r", bufs=4))
-        ps_a = ctx.enter_context(tc.psum_pool(name="ps_a", bufs=4))
+        small = ctx.enter_context(tc.tile_pool(name="small", bufs=2))
+        gates = ctx.enter_context(tc.tile_pool(name="gates", bufs=9))
+        psum = ctx.enter_context(tc.psum_pool(name="psum", bufs=2))
 
         ident_f = const.tile([P, P], F32, name="ident_f")
         make_identity(nc, ident_f[:])
@@ -92,17 +91,14 @@ def tile_multilstm_pa_t_kernel(
                 grouped = stg.tile([P, ST * P * 4], BF16, name="grouped", tag="grouped", align_bytes=64)
                 g_words = grouped[:].bitcast(F32).rearrange("p (t c u) -> p t c u", t=ST, u=2)
                 for half in range(2):
-                    bank = ps_a.tile([P, 2, 2, P], F32, name="tp_w", tag="ap")
+                    bank = psum.tile([P, 2, 2, P], F32, name="tp_w", tag="r", bufs=4)
                     for i in range(2):
                         for u in range(2):
                             col = (2 * half + i) * (H // 2) + u * P
                             nc.tensor.transpose(bank[:, i, u, :], words[:, col:col + P], ident_f[:])
-                    src_v = bank[:].rearrange("p t u c -> p t c u")
-                    dst_v = g_words[:, 2 * half:2 * half + 2, :, :]
-                    if half == 0:
-                        nc.vector.tensor_copy(out=dst_v, in_=src_v)
-                    else:
-                        nc.scalar.copy(out=dst_v, in_=src_v)
+                    nc.scalar.copy(
+                        out=g_words[:, 2 * half:2 * half + 2, :, :], in_=bank[:].rearrange("p t u c -> p t c u")
+                    )
                 nc.vector.quantize_mx(out=codes.bitcast(FP8X4), scales=scales, in_=grouped[:])
 
             for g in range(4):
@@ -112,23 +108,23 @@ def tile_multilstm_pa_t_kernel(
                 cols = slice(s * H, (s + 1) * H)
                 pack_rows(h0_v[:, ST * s:ST * (s + 1), :], h_codes[:, cols], h_scales[:, cols])
 
-            bank = ps_a.tile([P, P], BF16, name="tp_v", tag="ap")
+            bank = psum.tile([P, P], BF16, name="tp_v", tag="sa")
             nc.tensor.transpose(bank[:], vec[:], ident_b[:])
             nc.vector.tensor_copy(out=v_t[:], in_=bank[:, 0:48])
             nc.vector.tensor_tensor(out=b_t[:], in0=v_t[:, 16:32], in1=v_t[:, 32:48], op=ALU.add)
 
             for g in range(4):
-                bank = ps_a.tile([P, 4, P], BF16, name="tp_b", tag="ap")
+                bank = psum.tile([P, 4, P], BF16, name="tp_b", tag="sa")
                 for i in range(4):
                     nc.tensor.transpose(bank[:, i, :], w_n[:, 4 * g + i, :], ident_b[:])
                 nc.scalar.copy(out=w_t[:, 4 * g * P:4 * (g + 1) * P], in_=bank[:].rearrange("p t c -> p (t c)"))
             for g in range(NT // 4):
-                bank = ps_a.tile([P, 4, P], BF16, name="tp_b", tag="ap")
+                bank = psum.tile([P, 4, P], BF16, name="tp_b", tag="sa")
                 for i in range(4):
                     nc.tensor.transpose(bank[:, i, :], x_sb[:, 4 * g + i, :], ident_b[:])
                 nc.scalar.copy(out=x_t[:, 4 * g * P:4 * (g + 1) * P], in_=bank[:].rearrange("p t c -> p (t c)"))
 
-            g_ps = ps_a.tile([P, P + 2], F32, name="g_ps", tag="ap")
+            g_ps = psum.tile([P, P + 2], F32, name="g_ps", tag="vp")
             for t in range(16):
                 nc.tensor.matmul(g_ps[:, 0:P], lhsT=w_n[:, t, :], rhs=w_n[:, t, :], start=(t == 0), stop=(t == 15))
             for t in range(16):
@@ -138,30 +134,24 @@ def tile_multilstm_pa_t_kernel(
             nc.vector.tensor_copy(out=ws_hl[:, 0, :], in_=g_ps[:, P:P + 2])
             nc.vector.tensor_tensor(out=ws_hl[:, 1, :], in0=g_ps[:, P:P + 2], in1=ws_hl[:, 0, :], op=ALU.subtract)
 
-            m_ps = ps_r.tile([P, NT, 4], F32, name="m_ps", tag="r")
-            for g in range(NT // 2):
-                y_ps = ps_a.tile([P, 2, 2, P], F32, name="y_ps", tag="ap")
-                for i in range(2):
-                    t = 2 * g + i
+            m_ps = psum.tile([P, NT, 2], F32, name="m_ps", tag="sa")
+            for g in range(NT // 4):
+                y_ps = psum.tile([P, 4, P], F32, name="y_ps", tag="vp")
+                for i in range(4):
+                    t = 4 * g + i
                     lhs = x_t[:, t * P:(t + 1) * P]
-                    nc.tensor.matmul(
-                        y_ps[:, i, :, :].rearrange("p h v -> p (h v)"),
-                        lhsT=lhs,
-                        rhs=g_hl[:].rearrange("p h v -> p (h v)"),
-                        start=True,
-                        stop=True,
-                    )
-                    nc.tensor.matmul(
-                        m_ps[:, t, :], lhsT=lhs, rhs=ws_hl[:].rearrange("p h n -> p (h n)"), start=True, stop=True
-                    )
-                for i in range(2):
-                    t = 2 * g + i
-                    junk = pro.tile([P, 2, P], F32, name="junk", tag="junk", bufs=2)
+                    nc.tensor.matmul(y_ps[:, i, :], lhsT=lhs, rhs=g_hl[:, 0, :], start=True, stop=False)
+                    nc.tensor.matmul(y_ps[:, i, :], lhsT=lhs, rhs=g_hl[:, 1, :], start=False, stop=True)
+                    nc.tensor.matmul(m_ps[:, t, :], lhsT=lhs, rhs=ws_hl[:, 0, :], start=True, stop=False)
+                    nc.tensor.matmul(m_ps[:, t, :], lhsT=lhs, rhs=ws_hl[:, 1, :], start=False, stop=True)
+                for i in range(4):
+                    t = 4 * g + i
+                    junk = pro.tile([P, P], F32, name="junk", tag="junk", bufs=2)
                     nc.vector.scalar_tensor_tensor(
                         out=junk[:],
-                        in0=y_ps[:, i, :, :],
+                        in0=y_ps[:, i, :],
                         scalar=1.0,
-                        in1=x_sb[:, t, :].unsqueeze(1).to_broadcast([P, 2, P]),
+                        in1=x_sb[:, t, :],
                         op0=ALU.mult,
                         op1=ALU.mult,
                         accum_out=sumsq_a[:, t:t + 1],
@@ -180,17 +170,27 @@ def tile_multilstm_pa_t_kernel(
 
         work = ctx.enter_context(tc.tile_pool(name="work", bufs=2))
 
-        gt = {}
-        rs_r = {}
-        ahat = {}
-        p2t = {}
-        c0s = {}
+        r_bank, a_bank, t_bank, p_bank = {}, {}, {}, {}
+        gt, so, mv_r, rs_r, ahat, p2t, c0s = {}, {}, {}, {}, {}, {}, {}
+        c1s, c2s, ys, cys, tcs, mv_c, rs_c = {}, {}, {}, {}, {}, {}, {}
 
-        def r_phase(t):
-            banks = []
+        def inside(i):
+            return 0 <= i < NT
+
+        def rsqrt_eps(var, tag, bufs):
+            ve = small.tile([P, 1], F32, name="ve_" + tag, tag="ve_" + tag)
+            nc.gpsimd.tensor_scalar(out=ve[:], in0=var, scalar1=EPS, scalar2=1.0, op0=ALU.add, op1=ALU.mult)
+            rs = small.tile([P, 1], F32, name="rs_" + tag, tag="rs_" + tag, bufs=bufs)
+            nc.gpsimd.tensor_tensor(out=rs[:], in0=ve[:], in1=mhalf[:, 0:1], op=ALU.pow)
+            return rs
+
+        def mx(t):
+            if not inside(t):
+                return
             rows = slice(t * P, (t + 1) * P)
+            r_bank[t] = []
             for c in range(4):
-                bank = ps_r.tile([P, H], F32, name="r_ps", tag="r")
+                bank = psum.tile([P, H], F32, name="r_ps", tag="r", bufs=4)
                 cols = slice(c * H, (c + 1) * H)
                 nc.tensor.matmul_mx(
                     out=bank[:],
@@ -201,130 +201,223 @@ def tile_multilstm_pa_t_kernel(
                     start=True,
                     stop=True,
                 )
-                banks.append(bank)
-            st = small.tile([P, 4, 6], F32, name="st_r", tag="st_r")
-            for c in range(4):
-                nc.vector.bn_stats(out=st[:, c, :], in_=banks[c][:])
-            mv = small.tile([P, 2], F32, name="mv_r", tag="mv_r")
-            nc.vector.bn_aggr(out=mv[:], in_=st[:].rearrange("p c s -> p (c s)"))
-            ve = small.tile([P, 1], F32, name="ve_r", tag="ve_r")
-            nc.vector.tensor_scalar(out=ve[:], in0=mv[:, 1:2], scalar1=EPS, scalar2=None, op0=ALU.add)
-            rs = small.tile([P, 1], F32, name="rs_r", tag="rs_r", bufs=12)
-            nc.gpsimd.tensor_tensor(out=rs[:], in0=ve[:], in1=mhalf[:, 0:1], op=ALU.pow)
-            rs_r[t] = rs
-            gate = gates.tile([P, G], F32, name="gate", tag="gate")
-            for c in range(4):
-                cols = slice(c * H, (c + 1) * H)
-                nc.vector.scalar_tensor_tensor(
-                    out=gate[:, cols],
-                    in0=banks[c][:],
-                    scalar=mv[:, 0:1],
-                    in1=wh_bc[:, cols],
-                    op0=ALU.subtract,
-                    op1=ALU.mult,
-                )
-            gt[t] = gate
+                r_bank[t].append(bank)
 
-        def a1(k):
-            s, c = divmod(k, 4)
+        def st(t):
+            if not inside(t):
+                return
+            st6 = small.tile([P, 4, 6], F32, name="st_r", tag="st_r")
+            for c in range(4):
+                nc.vector.bn_stats(out=st6[:, c, :], in_=r_bank[t][c][:])
+            mv = small.tile([P, 2], F32, name="mv_r", tag="mv_r", bufs=3)
+            nc.vector.bn_aggr(out=mv[:], in_=st6[:].rearrange("p c s -> p (c s)"))
+            mv_r[t] = mv
+            rs_r[t] = rsqrt_eps(mv[:, 1:2], "r", 10)
+
+        def q(t, c):
+            if not inside(t):
+                return
             if c == 0:
-                c0_sb = work.tile([P, ST, H], BF16, name="c0_sb", tag="c0_sb", bufs=3)
-                nc.sync.dma_start(out=c0_sb[:], in_=c0_v[:, ST * s:ST * (s + 1), :])
-                c0s[s] = c0_sb
-            ah = work.tile([P, ST, H], F32, name="ahat", tag="ahat")
-            for bt in range(ST):
-                t = ST * s + bt
-                bank = ps_a.tile([P, H], F32, name="a_ps", tag="ap")
-                nc.tensor.matmul(
-                    bank[:], lhsT=x_t[:, t * P:(t + 1) * P], rhs=w_t[:, c * H:(c + 1) * H], start=True, stop=True
-                )
-                nc.scalar.activation(
-                    out=ah[:, bt, :], in_=bank[:], func=ACT.Identity, bias=nb_a[:, t:t + 1], scale=rs_a[:, t:t + 1]
-                )
-            ahat[k] = ah
+                gt[t] = gates.tile([P, G], F32, name="gate", tag="gate")
+            cols = slice(c * H, (c + 1) * H)
+            nc.vector.scalar_tensor_tensor(
+                out=gt[t][:, cols],
+                in0=r_bank[t][c][:],
+                scalar=mv_r[t][:, 0:1],
+                in1=wh_bc[:, cols],
+                op0=ALU.subtract,
+                op1=ALU.mult,
+            )
 
-        def a2(k):
-            c = k % 4
-            ah = ahat[k]
-            pt = work.tile([P, 4, ST * P], F32, name="p2t", tag="p2t")
+        def am(k, bt):
+            if not inside(k):
+                return
+            s, c = divmod(k, 4)
+            t = ST * s + bt
+            bank = psum.tile([P, H], F32, name="a_ps", tag="sa")
+            nc.tensor.matmul(
+                bank[:], lhsT=x_t[:, t * P:(t + 1) * P], rhs=w_t[:, c * H:(c + 1) * H], start=True, stop=True
+            )
+            a_bank[(k, bt)] = bank
+
+        def ah(k, bt):
+            if not inside(k):
+                return
+            t = ST * (k // 4) + bt
+            if bt == 0:
+                ahat[k] = work.tile([P, ST, H], F32, name="ahat", tag="ahat")
+            nc.scalar.activation(
+                out=ahat[k][:, bt, :],
+                in_=a_bank[(k, bt)][:],
+                func=ACT.Identity,
+                bias=nb_a[:, t:t + 1],
+                scale=rs_a[:, t:t + 1],
+            )
+
+        def tb(k, jb):
+            if not inside(k):
+                return
+            bank = psum.tile([P, ST, P], F32, name="t_ps", tag="sa")
+            for bt in range(ST):
+                nc.tensor.transpose(bank[:, bt, :], ahat[k][:, bt, jb * P:(jb + 1) * P], ident_f[:])
+            t_bank[(k, jb)] = bank
+
+        def pt(k, jb):
+            if not inside(k):
+                return
+            if jb == 0:
+                p2t[k] = work.tile([P, 4, ST * P], F32, name="p2t", tag="p2t")
+            col = 4 * (k % 4) + jb
+            nc.scalar.activation(
+                out=p2t[k][:, jb, :],
+                in_=t_bank[(k, jb)][:].rearrange("p t b -> p (t b)"),
+                func=ACT.Identity,
+                bias=b_t[:, col:col + 1],
+                scale=v_t[:, col:col + 1],
+            )
+
+        def p2(k, bt):
+            if not inside(k):
+                return
+            bank = psum.tile([P, 4, P], F32, name="p_ps", tag="vp")
             for jb in range(4):
-                bank = ps_a.tile([P, ST, P], F32, name="t_ps", tag="ap")
-                for bt in range(ST):
-                    nc.tensor.transpose(bank[:, bt, :], ah[:, bt, jb * P:(jb + 1) * P], ident_f[:])
-                col = 4 * c + jb
-                nc.scalar.activation(
-                    out=pt[:, jb, :],
-                    in_=bank[:].rearrange("p t b -> p (t b)"),
-                    func=ACT.Identity,
-                    bias=b_t[:, col:col + 1],
-                    scale=v_t[:, col:col + 1],
-                )
-            p2t[k] = pt
+                nc.tensor.transpose(bank[:, jb, :], p2t[k][:, jb, bt * P:(bt + 1) * P], ident_f[:])
+            p_bank[(k, bt)] = bank
 
-        def a3(k):
+        def z(k, bt):
+            if not inside(k):
+                return
             s, c = divmod(k, 4)
-            pt = p2t[k]
-            for bt in range(ST):
-                t = ST * s + bt
-                bank = ps_a.tile([P, 4, P], F32, name="p_ps", tag="ap")
-                for jb in range(4):
-                    nc.tensor.transpose(bank[:, jb, :], pt[:, jb, bt * P:(bt + 1) * P], ident_f[:])
-                dst = gt[t][:, c * H:(c + 1) * H]
-                nc.vector.scalar_tensor_tensor(
-                    out=dst,
-                    in0=dst,
-                    scalar=rs_r[t][:, 0:1],
-                    in1=bank[:].rearrange("p j c -> p (j c)"),
-                    op0=ALU.mult,
-                    op1=ALU.add,
-                )
+            t = ST * s + bt
+            dst = gt[t][:, c * H:(c + 1) * H]
+            nc.vector.scalar_tensor_tensor(
+                out=dst,
+                in0=dst,
+                scalar=rs_r[t][:, 0:1],
+                in1=p_bank[(k, bt)][:].rearrange("p j c -> p (j c)"),
+                op0=ALU.mult,
+                op1=ALU.add,
+            )
 
-        def a4(k):
+        def act(k, bt):
+            if not inside(k):
+                return
             s, c = divmod(k, 4)
-            for bt in range(ST):
-                dst = gt[ST * s + bt][:, c * H:(c + 1) * H]
-                nc.scalar.activation(out=dst, in_=dst, func=(ACT.Tanh if c == 2 else ACT.Sigmoid))
+            t = ST * s + bt
+            src = gt[t][:, c * H:(c + 1) * H]
+            if c == 3:
+                so[t] = work.tile([P, H], F32, name="so", tag="so", bufs=8)
+                nc.scalar.activation(out=so[t][:], in_=src, func=ACT.Sigmoid)
+            else:
+                nc.scalar.activation(out=src, in_=src, func=(ACT.Tanh if c == 2 else ACT.Sigmoid))
 
-        def cell(t):
+        def pair_engine(t):
+            return nc.vector if t >= NT - ST else nc.gpsimd
+
+        def c12(t):
+            if not inside(t):
+                return
             s, bt = divmod(t, ST)
-            gate = gt[t]
-            c1 = work.tile([P, H], F32, name="c1", tag="c1")
-            c2 = work.tile([P, H], F32, name="c2", tag="c2")
-            nc.gpsimd.tensor_tensor(out=c1[:], in0=gate[:, H:2 * H], in1=c0s[s][:, bt, :], op=ALU.mult)
-            nc.gpsimd.tensor_tensor(out=c2[:], in0=gate[:, 0:H], in1=gate[:, 2 * H:3 * H], op=ALU.mult)
-            nc.gpsimd.tensor_tensor(out=c1[:], in0=c1[:], in1=c2[:], op=ALU.add)
-            st = small.tile([P, 6], F32, name="st_c", tag="st_c")
-            nc.vector.bn_stats(out=st[:], in_=c1[:])
-            mv = small.tile([P, 2], F32, name="mv_c", tag="mv_c")
-            nc.vector.bn_aggr(out=mv[:], in_=st[:])
-            ve = small.tile([P, 1], F32, name="ve_c", tag="ve_c")
-            nc.vector.tensor_scalar(out=ve[:], in0=mv[:, 1:2], scalar1=EPS, scalar2=None, op0=ALU.add)
-            rs = small.tile([P, 1], F32, name="rs_c", tag="rs_c")
-            nc.gpsimd.tensor_tensor(out=rs[:], in0=ve[:], in1=mhalf[:, 0:1], op=ALU.pow)
+            c1s[t] = work.tile([P, H], F32, name="c1", tag="c1", bufs=3)
+            c2s[t] = work.tile([P, H], F32, name="c2", tag="c2")
+            eng = pair_engine(t)
+            eng.tensor_tensor(out=c1s[t][:], in0=gt[t][:, H:2 * H], in1=c0s[s][:, bt, :], op=ALU.mult)
+            eng.tensor_tensor(out=c2s[t][:], in0=gt[t][:, 0:H], in1=gt[t][:, 2 * H:3 * H], op=ALU.mult)
+
+        def csum(t):
+            if not inside(t):
+                return
+            pair_engine(t).tensor_tensor(out=c1s[t][:], in0=c1s[t][:], in1=c2s[t][:], op=ALU.add)
+
+        def cstat(t):
+            if not inside(t):
+                return
+            st6 = small.tile([P, 6], F32, name="st_c", tag="st_c")
+            nc.vector.bn_stats(out=st6[:], in_=c1s[t][:])
+            mv = small.tile([P, 2], F32, name="mv_c", tag="mv_c", bufs=3)
+            nc.vector.bn_aggr(out=mv[:], in_=st6[:])
+            mv_c[t] = mv
+
+        def cpow(t):
+            if not inside(t):
+                return
+            rs_c[t] = rsqrt_eps(mv_c[t][:, 1:2], "c", 3)
+
+        def yop(t):
+            if not inside(t):
+                return
+            ys[t] = work.tile([P, H], F32, name="y", tag="y")
             nc.vector.scalar_tensor_tensor(
-                out=c2[:], in0=c1[:], scalar=mv[:, 0:1], in1=cw_bc[:], op0=ALU.subtract, op1=ALU.mult
+                out=ys[t][:], in0=c1s[t][:], scalar=mv_c[t][:, 0:1], in1=cw_bc[:], op0=ALU.subtract, op1=ALU.mult
             )
-            cy = work.tile([P, H], F32, name="cy", tag="cy", bufs=3)
+
+        def cyop(t):
+            if not inside(t):
+                return
+            cys[t] = work.tile([P, H], F32, name="cy", tag="cy", bufs=3)
             nc.vector.scalar_tensor_tensor(
-                out=cy[:], in0=c2[:], scalar=rs[:, 0:1], in1=cb_bc[:], op0=ALU.mult, op1=ALU.add
+                out=cys[t][:], in0=ys[t][:], scalar=rs_c[t][:, 0:1], in1=cb_bc[:], op0=ALU.mult, op1=ALU.add
             )
-            nc.sync.dma_start(out=cy_v[:, t, :], in_=cy[:])
-            tcy = work.tile([P, H], F32, name="tcy", tag="tcy")
-            nc.scalar.activation(out=tcy[:], in_=cy[:], func=ACT.Tanh)
+            nc.sync.dma_start(out=cy_v[:, t, :], in_=cys[t][:])
+
+        def th(t):
+            if not inside(t):
+                return
+            tcs[t] = work.tile([P, H], F32, name="tcy", tag="tcy", bufs=3)
+            nc.scalar.activation(out=tcs[t][:], in_=cys[t][:], func=ACT.Tanh)
+
+        def hyop(t):
+            if not inside(t):
+                return
             hy = work.tile([P, H], F32, name="hy", tag="hy", bufs=3)
-            nc.gpsimd.tensor_tensor(out=hy[:], in0=gate[:, 3 * H:4 * H], in1=tcy[:], op=ALU.mult)
+            eng = nc.vector if t >= NT - 2 * ST else nc.gpsimd
+            eng.tensor_tensor(out=hy[:], in0=so[t][:], in1=tcs[t][:], op=ALU.mult)
             nc.sync.dma_start(out=hy_v[:, t, :], in_=hy[:])
 
-        for n in range(-4, NT + 5):
-            if 0 <= n - 5 < NT:
-                cell(n - 5)
-            if 0 <= n - 1 < NT:
-                a4(n - 1)
-            if 0 <= n < NT:
-                a3(n)
-            if 0 <= n + 1 < NT:
-                a2(n + 1)
-            if 0 <= n + 2 < NT:
-                a1(n + 2)
-            if 0 <= n + 4 < NT:
-                r_phase(n + 4)
+        with tc.manual_schedule():
+            for n in range(-5, NT + 9):
+                if n % ST == 0 and inside(n):
+                    c0s[n // ST] = work.tile([P, ST, H], BF16, name="c0_sb", tag="c0_sb", bufs=3)
+                    nc.sync.dma_start(out=c0s[n // ST][:], in_=c0_v[:, n:n + ST, :])
+                p2(n, 0)
+                p2(n, 1)
+                c12(n - 4)
+                st(n + 4)
+                ah(n + 2, 0)
+                act(n - 1, 0)
+                am(n + 2, 2)
+                ah(n + 2, 1)
+                act(n - 1, 1)
+                am(n + 2, 3)
+                z(n, 0)
+                p2(n, 2)
+                z(n, 1)
+                p2(n, 3)
+                ah(n + 2, 2)
+                act(n - 1, 2)
+                tb(n + 1, 0)
+                ah(n + 2, 3)
+                act(n - 1, 3)
+                tb(n + 1, 1)
+                q(n + 4, 0)
+                q(n + 4, 1)
+                csum(n - 4)
+                pt(n + 1, 0)
+                th(n - 7)
+                tb(n + 1, 2)
+                pt(n + 1, 1)
+                tb(n + 1, 3)
+                z(n, 2)
+                z(n, 3)
+                q(n + 4, 2)
+                q(n + 4, 3)
+                pt(n + 1, 2)
+                am(n + 3, 0)
+                pt(n + 1, 3)
+                am(n + 3, 1)
+                mx(n + 5)
+                hyop(n - 8)
+                cstat(n - 5)
+                cyop(n - 6)
+                yop(n - 5)
+                cpow(n - 5)

@@ -91,7 +91,7 @@ def tile_multilstm_pa_t_kernel(
                 grouped = stg.tile([P, ST * P * 4], BF16, name="grouped", tag="grouped", align_bytes=64)
                 g_words = grouped[:].bitcast(F32).rearrange("p (t c u) -> p t c u", t=ST, u=2)
                 for half in range(2):
-                    bank = psum.tile([P, 2, 2, P], F32, name="tp_w", tag="r", bufs=4)
+                    bank = psum.tile([P, 2, 2, P], F32, name="tp_w", tag="vs", bufs=4)
                     for i in range(2):
                         for u in range(2):
                             col = (2 * half + i) * (H // 2) + u * P
@@ -108,23 +108,23 @@ def tile_multilstm_pa_t_kernel(
                 cols = slice(s * H, (s + 1) * H)
                 pack_rows(h0_v[:, ST * s:ST * (s + 1), :], h_codes[:, cols], h_scales[:, cols])
 
-            bank = psum.tile([P, P], BF16, name="tp_v", tag="sa")
+            bank = psum.tile([P, P], BF16, name="tp_v", tag="ss", bufs=4)
             nc.tensor.transpose(bank[:], vec[:], ident_b[:])
             nc.vector.tensor_copy(out=v_t[:], in_=bank[:, 0:48])
             nc.vector.tensor_tensor(out=b_t[:], in0=v_t[:, 16:32], in1=v_t[:, 32:48], op=ALU.add)
 
             for g in range(4):
-                bank = psum.tile([P, 4, P], BF16, name="tp_b", tag="sa")
+                bank = psum.tile([P, 4, P], BF16, name="tp_b", tag="ss", bufs=4)
                 for i in range(4):
                     nc.tensor.transpose(bank[:, i, :], w_n[:, 4 * g + i, :], ident_b[:])
                 nc.scalar.copy(out=w_t[:, 4 * g * P:4 * (g + 1) * P], in_=bank[:].rearrange("p t c -> p (t c)"))
             for g in range(NT // 4):
-                bank = psum.tile([P, 4, P], BF16, name="tp_b", tag="sa")
+                bank = psum.tile([P, 4, P], BF16, name="tp_b", tag="ss", bufs=4)
                 for i in range(4):
                     nc.tensor.transpose(bank[:, i, :], x_sb[:, 4 * g + i, :], ident_b[:])
                 nc.scalar.copy(out=x_t[:, 4 * g * P:4 * (g + 1) * P], in_=bank[:].rearrange("p t c -> p (t c)"))
 
-            g_ps = psum.tile([P, P + 2], F32, name="g_ps", tag="vp")
+            g_ps = psum.tile([P, P + 2], F32, name="g_ps", tag="ss", bufs=4)
             for t in range(16):
                 nc.tensor.matmul(g_ps[:, 0:P], lhsT=w_n[:, t, :], rhs=w_n[:, t, :], start=(t == 0), stop=(t == 15))
             for t in range(16):
@@ -134,9 +134,9 @@ def tile_multilstm_pa_t_kernel(
             nc.vector.tensor_copy(out=ws_hl[:, 0, :], in_=g_ps[:, P:P + 2])
             nc.vector.tensor_tensor(out=ws_hl[:, 1, :], in0=g_ps[:, P:P + 2], in1=ws_hl[:, 0, :], op=ALU.subtract)
 
-            m_ps = psum.tile([P, NT, 2], F32, name="m_ps", tag="sa")
+            m_ps = psum.tile([P, NT, 2], F32, name="m_ps", tag="ss", bufs=4)
             for g in range(NT // 4):
-                y_ps = psum.tile([P, 4, P], F32, name="y_ps", tag="vp")
+                y_ps = psum.tile([P, 4, P], F32, name="y_ps", tag="ss", bufs=4)
                 for i in range(4):
                     t = 4 * g + i
                     lhs = x_t[:, t * P:(t + 1) * P]
@@ -170,7 +170,7 @@ def tile_multilstm_pa_t_kernel(
 
         work = ctx.enter_context(tc.tile_pool(name="work", bufs=2))
 
-        r_bank, a_bank, t_bank, p_bank = {}, {}, {}, {}
+        s_bank, q_bank, st_r, a_bank, t_bank, p_bank = {}, {}, {}, {}, {}, {}
         gt, so, mv_r, rs_r, ahat, p2t, c0s = {}, {}, {}, {}, {}, {}, {}
         c1s, c2s, ys, cys, tcs, mv_c, rs_c = {}, {}, {}, {}, {}, {}, {}
 
@@ -184,37 +184,45 @@ def tile_multilstm_pa_t_kernel(
             nc.gpsimd.tensor_tensor(out=rs[:], in0=ve[:], in1=mhalf[:, 0:1], op=ALU.pow)
             return rs
 
-        def mx(t):
-            if not inside(t):
-                return
+        def r_pass(t, c):
             rows = slice(t * P, (t + 1) * P)
-            r_bank[t] = []
-            for c in range(4):
-                bank = psum.tile([P, H], F32, name="r_ps", tag="r", bufs=4)
-                cols = slice(c * H, (c + 1) * H)
-                nc.tensor.matmul_mx(
-                    out=bank[:],
-                    lhsT=h_codes[:, rows].bitcast(FP8X4),
-                    lhsT_scale=h_scales[:, rows],
-                    rhs=w_codes[:, cols].bitcast(FP8X4),
-                    rhs_scale=w_scales[:, cols],
-                    start=True,
-                    stop=True,
-                )
-                r_bank[t].append(bank)
+            cols = slice(c * H, (c + 1) * H)
+            bank = psum.tile([P, H], F32, name="r_ps", tag="vs", bufs=4)
+            nc.tensor.matmul_mx(
+                out=bank[:],
+                lhsT=h_codes[:, rows].bitcast(FP8X4),
+                lhsT_scale=h_scales[:, rows],
+                rhs=w_codes[:, cols].bitcast(FP8X4),
+                rhs_scale=w_scales[:, cols],
+                start=True,
+                stop=True,
+            )
+            return bank
 
-        def st(t):
+        def fill_st(t, c):
+            if inside(t):
+                s_bank[(t, c)] = r_pass(t, c)
+
+        def fill_q(t, c):
+            if inside(t):
+                q_bank[(t, c)] = r_pass(t, c)
+
+        def rd_st(t, c):
             if not inside(t):
                 return
-            st6 = small.tile([P, 4, 6], F32, name="st_r", tag="st_r")
-            for c in range(4):
-                nc.vector.bn_stats(out=st6[:, c, :], in_=r_bank[t][c][:])
-            mv = small.tile([P, 2], F32, name="mv_r", tag="mv_r", bufs=3)
-            nc.vector.bn_aggr(out=mv[:], in_=st6[:].rearrange("p c s -> p (c s)"))
-            mv_r[t] = mv
-            rs_r[t] = rsqrt_eps(mv[:, 1:2], "r", 10)
+            if c == 0:
+                st_r[t] = small.tile([P, 4, 6], F32, name="st_r", tag="st_r")
+            nc.vector.bn_stats(out=st_r[t][:, c, :], in_=s_bank[(t, c)][:])
 
-        def q(t, c):
+        def aggr(t):
+            if not inside(t):
+                return
+            mv = small.tile([P, 2], F32, name="mv_r", tag="mv_r", bufs=3)
+            nc.vector.bn_aggr(out=mv[:], in_=st_r[t][:].rearrange("p c s -> p (c s)"))
+            mv_r[t] = mv
+            rs_r[t] = rsqrt_eps(mv[:, 1:2], "r", 11)
+
+        def rd_q(t, c):
             if not inside(t):
                 return
             if c == 0:
@@ -222,7 +230,7 @@ def tile_multilstm_pa_t_kernel(
             cols = slice(c * H, (c + 1) * H)
             nc.vector.scalar_tensor_tensor(
                 out=gt[t][:, cols],
-                in0=r_bank[t][c][:],
+                in0=q_bank[(t, c)][:],
                 scalar=mv_r[t][:, 0:1],
                 in1=wh_bc[:, cols],
                 op0=ALU.subtract,
@@ -234,7 +242,7 @@ def tile_multilstm_pa_t_kernel(
                 return
             s, c = divmod(k, 4)
             t = ST * s + bt
-            bank = psum.tile([P, H], F32, name="a_ps", tag="sa")
+            bank = psum.tile([P, H], F32, name="a_ps", tag="ss", bufs=4)
             nc.tensor.matmul(
                 bank[:], lhsT=x_t[:, t * P:(t + 1) * P], rhs=w_t[:, c * H:(c + 1) * H], start=True, stop=True
             )
@@ -257,7 +265,7 @@ def tile_multilstm_pa_t_kernel(
         def tb(k, jb):
             if not inside(k):
                 return
-            bank = psum.tile([P, ST, P], F32, name="t_ps", tag="sa")
+            bank = psum.tile([P, ST, P], F32, name="t_ps", tag="ss", bufs=4)
             for bt in range(ST):
                 nc.tensor.transpose(bank[:, bt, :], ahat[k][:, bt, jb * P:(jb + 1) * P], ident_f[:])
             t_bank[(k, jb)] = bank
@@ -279,7 +287,7 @@ def tile_multilstm_pa_t_kernel(
         def p2(k, bt):
             if not inside(k):
                 return
-            bank = psum.tile([P, 4, P], F32, name="p_ps", tag="vp")
+            bank = psum.tile([P, 4, P], F32, name="p_ps", tag="vs", bufs=4)
             for jb in range(4):
                 nc.tensor.transpose(bank[:, jb, :], p2t[k][:, jb, bt * P:(bt + 1) * P], ident_f[:])
             p_bank[(k, bt)] = bank
@@ -375,49 +383,34 @@ def tile_multilstm_pa_t_kernel(
             nc.sync.dma_start(out=hy_v[:, t, :], in_=hy[:])
 
         with tc.manual_schedule():
-            for n in range(-5, NT + 9):
+            for n in range(-6, NT + 9):
                 if n % ST == 0 and inside(n):
                     c0s[n // ST] = work.tile([P, ST, H], BF16, name="c0_sb", tag="c0_sb", bufs=3)
                     nc.sync.dma_start(out=c0s[n // ST][:], in_=c0_v[:, n:n + ST, :])
-                p2(n, 0)
-                p2(n, 1)
-                c12(n - 4)
-                st(n + 4)
-                ah(n + 2, 0)
-                act(n - 1, 0)
-                am(n + 2, 2)
-                ah(n + 2, 1)
-                act(n - 1, 1)
-                am(n + 2, 3)
-                z(n, 0)
-                p2(n, 2)
-                z(n, 1)
-                p2(n, 3)
-                ah(n + 2, 2)
-                act(n - 1, 2)
-                tb(n + 1, 0)
-                ah(n + 2, 3)
-                act(n - 1, 3)
-                tb(n + 1, 1)
-                q(n + 4, 0)
-                q(n + 4, 1)
-                csum(n - 4)
-                pt(n + 1, 0)
-                th(n - 7)
-                tb(n + 1, 2)
-                pt(n + 1, 1)
-                tb(n + 1, 3)
-                z(n, 2)
-                z(n, 3)
-                q(n + 4, 2)
-                q(n + 4, 3)
-                pt(n + 1, 2)
-                am(n + 3, 0)
-                pt(n + 1, 3)
-                am(n + 3, 1)
-                mx(n + 5)
-                hyop(n - 8)
-                cstat(n - 5)
-                cyop(n - 6)
-                yop(n - 5)
-                cpow(n - 5)
+                for i in range(4):
+                    n1, i1 = divmod(4 * n + i + 1, 4)
+                    n2, i2 = divmod(4 * n + i + 2, 4)
+                    ah(n + 2, i)
+                    tb(n1 + 1, i1)
+                    pt(n + 1, i)
+                    am(n2 + 2, i2)
+                    act(n - 1, i)
+                    fill_st(n1 + 5, i1)
+                    rd_st(n + 5, i)
+                    fill_q(n1 + 4, i1)
+                    rd_q(n + 4, i)
+                    p2(n1, i1)
+                    z(n, i)
+                    if i == 0:
+                        c12(n - 4)
+                        cstat(n - 5)
+                    elif i == 1:
+                        cpow(n - 5)
+                        csum(n - 4)
+                        cyop(n - 6)
+                        th(n - 7)
+                    elif i == 2:
+                        yop(n - 5)
+                        hyop(n - 8)
+                    else:
+                        aggr(n + 5)

@@ -20,6 +20,52 @@ ST = 4
 EPS = 1e-5
 FLOPS = 2 * B * G * (H + V)
 
+RAW_BUFS = 5
+GROUPED_BUFS = 5
+
+C1_BUFS = 6
+C2_BUFS = 3
+LAST_SLOT = NT + 1
+
+
+def CELL_PLAN():
+    plan = {}
+
+    def put(n, i, name, t, on_vector=False):
+        if (n, i) not in plan:
+            plan[(n, i)] = []
+        plan[(n, i)].append((name, t, on_vector))
+
+    for t in range(NT - 2 * ST):
+        put(t + 4, 0, "c1", t)
+        put(t + 4, 0, "c2", t)
+        put(t + 5, 0, "cstat", t)
+        put(t + 5, 1, "cpow", t)
+        put(t + 4, 1, "csum", t)
+        put(t + 5, 1, "y", t)
+        put(t + 5, 2, "cy", t)
+        put(t + 6, 2, "hy", t)
+        put(t + 5, 3, "th", t)
+    for j, t in enumerate(range(NT - 2 * ST, NT - ST)):
+        n = NT - ST + j // 2
+        v = j % 2 == 1
+        put(n, 0 + v, "c1", t, v)
+        put(n, 0 + v, "c2", t, v)
+        put(n, 1 + v, "csum", t, v)
+        put(n + 1, 0 + v, "cstat", t)
+        put(n + 1, 1 + v, "cpow", t)
+        put(n + 1, 1 + v, "y", t)
+        put(n + 1, 2 + v, "cy", t)
+        put(n + 2, 0 + v, "th", t)
+        put(n + 2, 2 + v, "hy", t, True)
+    for j, t in enumerate(range(NT - ST, NT)):
+        m = 4 * (NT - 1) + j
+        put((m - 2) // 4, (m - 2) % 4, "c1", t)
+        for d, names in ((1, ("c2", "csum", "cstat")), (2, ("cpow", "y")), (3, ("cy",)), (4, ("th",)), (5, ("hy",))):
+            for name in names:
+                put((m + d) // 4, (m + d) % 4, name, t, True)
+    return plan
+
 
 def tile_multilstm_pa_t_kernel(
     tc, x, h0, c0, w_ih1, w_hh1, lni_w1, lni_b1, lnh_w1, lnh_b1, lnc_w1, lnc_b1, out_0, out_1
@@ -37,7 +83,9 @@ def tile_multilstm_pa_t_kernel(
         const = ctx.enter_context(tc.tile_pool(name="const", bufs=1))
         small = ctx.enter_context(tc.tile_pool(name="small", bufs=2))
         gates = ctx.enter_context(tc.tile_pool(name="gates", bufs=9))
-        psum = ctx.enter_context(tc.psum_pool(name="psum", bufs=2))
+        work = ctx.enter_context(tc.tile_pool(name="work", bufs=2))
+        psum = ctx.enter_context(tc.psum_pool(name="psum", bufs=4))
+        cellp = []
 
         ident_f = const.tile([P, P], F32, name="ident_f")
         make_identity(nc, ident_f[:])
@@ -57,8 +105,7 @@ def tile_multilstm_pa_t_kernel(
         wh_bc = const.tile([P, G], BF16, name="wh_bc")
         cw_bc = const.tile([P, H], BF16, name="cw_bc")
         cb_bc = const.tile([P, H], BF16, name="cb_bc")
-        g_hl = const.tile([P, 2, P], BF16, name="g_hl")
-        ws_hl = const.tile([P, 2, 2], BF16, name="ws_hl")
+        g_hl = const.tile([P, 2, P + 2], BF16, name="g_hl")
         v_t = const.tile([P, 48], F32, name="v_t")
         b_t = const.tile([P, 16], F32, name="b_t")
         sum_a = const.tile([P, NT], F32, name="sum_a")
@@ -69,106 +116,6 @@ def tile_multilstm_pa_t_kernel(
         ve_a = const.tile([P, NT], F32, name="ve_a")
         rs_a = const.tile([P, NT], F32, name="rs_a")
         nb_a = const.tile([P, NT], F32, name="nb_a")
-
-        with tc.tile_pool(name="pro", bufs=1) as pro, tc.tile_pool(name="stage", bufs=3) as stg:
-            x_sb = pro.tile([P, NT, V], BF16, name="x_sb")
-            w_n = pro.tile([P, 16, V], BF16, name="w_n")
-            vec = pro.tile([P, P], BF16, name="vec")
-            nc.vector.memset(vec[:], 0.0)
-            nc.scalar.dma_start(out=w_n[:], in_=wih_v)
-            nc.scalar.dma_start(out=x_sb[:], in_=x_v)
-            nc.scalar.dma_start(out=vec[0:16, :], in_=lni_w1.rearrange("(t p) -> t p", p=P))
-            nc.scalar.dma_start(out=vec[16:32, :], in_=lni_b1.rearrange("(t p) -> t p", p=P))
-            nc.scalar.dma_start(out=vec[32:48, :], in_=lnh_b1.rearrange("(t p) -> t p", p=P))
-            nc.scalar.dma_start(out=wh_bc[:], in_=lnh_w1.partition_broadcast(P))
-            nc.scalar.dma_start(out=cw_bc[:], in_=lnc_w1.partition_broadcast(P))
-            nc.scalar.dma_start(out=cb_bc[:], in_=lnc_b1.partition_broadcast(P))
-
-            def pack_rows(src, codes, scales):
-                raw = stg.tile([P, ST * H], BF16, name="raw", tag="raw")
-                nc.sync.dma_start(out=raw[:].rearrange("p (t k) -> p t k", t=ST), in_=src)
-                words = raw[:].bitcast(F32)
-                grouped = stg.tile([P, ST * P * 4], BF16, name="grouped", tag="grouped", align_bytes=64)
-                g_words = grouped[:].bitcast(F32).rearrange("p (t c u) -> p t c u", t=ST, u=2)
-                for half in range(2):
-                    bank = psum.tile([P, 2, 2, P], F32, name="tp_w", tag="vs", bufs=4)
-                    for i in range(2):
-                        for u in range(2):
-                            col = (2 * half + i) * (H // 2) + u * P
-                            nc.tensor.transpose(bank[:, i, u, :], words[:, col:col + P], ident_f[:])
-                    nc.scalar.copy(
-                        out=g_words[:, 2 * half:2 * half + 2, :, :], in_=bank[:].rearrange("p t u c -> p t c u")
-                    )
-                nc.vector.quantize_mx(out=codes.bitcast(FP8X4), scales=scales, in_=grouped[:])
-
-            for g in range(4):
-                cols = slice(g * H, (g + 1) * H)
-                pack_rows(whh_v[:, ST * g:ST * (g + 1), :], w_codes[:, cols], w_scales[:, cols])
-            for s in range(NT // ST):
-                cols = slice(s * H, (s + 1) * H)
-                pack_rows(h0_v[:, ST * s:ST * (s + 1), :], h_codes[:, cols], h_scales[:, cols])
-
-            bank = psum.tile([P, P], BF16, name="tp_v", tag="ss", bufs=4)
-            nc.tensor.transpose(bank[:], vec[:], ident_b[:])
-            nc.vector.tensor_copy(out=v_t[:], in_=bank[:, 0:48])
-            nc.vector.tensor_tensor(out=b_t[:], in0=v_t[:, 16:32], in1=v_t[:, 32:48], op=ALU.add)
-
-            for g in range(4):
-                bank = psum.tile([P, 4, P], BF16, name="tp_b", tag="ss", bufs=4)
-                for i in range(4):
-                    nc.tensor.transpose(bank[:, i, :], w_n[:, 4 * g + i, :], ident_b[:])
-                nc.scalar.copy(out=w_t[:, 4 * g * P:4 * (g + 1) * P], in_=bank[:].rearrange("p t c -> p (t c)"))
-            for g in range(NT // 4):
-                bank = psum.tile([P, 4, P], BF16, name="tp_b", tag="ss", bufs=4)
-                for i in range(4):
-                    nc.tensor.transpose(bank[:, i, :], x_sb[:, 4 * g + i, :], ident_b[:])
-                nc.scalar.copy(out=x_t[:, 4 * g * P:4 * (g + 1) * P], in_=bank[:].rearrange("p t c -> p (t c)"))
-
-            g_ps = psum.tile([P, P + 2], F32, name="g_ps", tag="ss", bufs=4)
-            for t in range(16):
-                nc.tensor.matmul(g_ps[:, 0:P], lhsT=w_n[:, t, :], rhs=w_n[:, t, :], start=(t == 0), stop=(t == 15))
-            for t in range(16):
-                nc.tensor.matmul(g_ps[:, P:P + 2], lhsT=w_n[:, t, :], rhs=ones_b[:], start=(t == 0), stop=(t == 15))
-            nc.vector.tensor_copy(out=g_hl[:, 0, :], in_=g_ps[:, 0:P])
-            nc.vector.tensor_tensor(out=g_hl[:, 1, :], in0=g_ps[:, 0:P], in1=g_hl[:, 0, :], op=ALU.subtract)
-            nc.vector.tensor_copy(out=ws_hl[:, 0, :], in_=g_ps[:, P:P + 2])
-            nc.vector.tensor_tensor(out=ws_hl[:, 1, :], in0=g_ps[:, P:P + 2], in1=ws_hl[:, 0, :], op=ALU.subtract)
-
-            m_ps = psum.tile([P, NT, 2], F32, name="m_ps", tag="ss", bufs=4)
-            for g in range(NT // 4):
-                y_ps = psum.tile([P, 4, P], F32, name="y_ps", tag="ss", bufs=4)
-                for i in range(4):
-                    t = 4 * g + i
-                    lhs = x_t[:, t * P:(t + 1) * P]
-                    nc.tensor.matmul(y_ps[:, i, :], lhsT=lhs, rhs=g_hl[:, 0, :], start=True, stop=False)
-                    nc.tensor.matmul(y_ps[:, i, :], lhsT=lhs, rhs=g_hl[:, 1, :], start=False, stop=True)
-                    nc.tensor.matmul(m_ps[:, t, :], lhsT=lhs, rhs=ws_hl[:, 0, :], start=True, stop=False)
-                    nc.tensor.matmul(m_ps[:, t, :], lhsT=lhs, rhs=ws_hl[:, 1, :], start=False, stop=True)
-                for i in range(4):
-                    t = 4 * g + i
-                    junk = pro.tile([P, P], F32, name="junk", tag="junk", bufs=2)
-                    nc.vector.scalar_tensor_tensor(
-                        out=junk[:],
-                        in0=y_ps[:, i, :],
-                        scalar=1.0,
-                        in1=x_sb[:, t, :],
-                        op0=ALU.mult,
-                        op1=ALU.mult,
-                        accum_out=sumsq_a[:, t:t + 1],
-                    )
-            nc.vector.tensor_reduce(out=sum_a[:], in_=m_ps[:], axis=AX.X, op=ALU.add)
-            nc.vector.tensor_scalar(out=mu_a[:], in0=sum_a[:], scalar1=1.0 / (2 * G), scalar2=None, op0=ALU.mult)
-            nc.vector.tensor_tensor(out=musq_a[:], in0=mu_a[:], in1=mu_a[:], op=ALU.mult)
-            nc.vector.scalar_tensor_tensor(
-                out=var_a[:], in0=sumsq_a[:], scalar=1.0 / G, in1=musq_a[:], op0=ALU.mult, op1=ALU.subtract
-            )
-            nc.vector.tensor_scalar(out=ve_a[:], in0=var_a[:], scalar1=0.0, scalar2=EPS, op0=ALU.max, op1=ALU.add)
-            nc.gpsimd.tensor_tensor(out=rs_a[:], in0=ve_a[:], in1=mhalf[:], op=ALU.pow)
-            nc.vector.scalar_tensor_tensor(
-                out=nb_a[:], in0=mu_a[:], scalar=-1.0, in1=rs_a[:], op0=ALU.mult, op1=ALU.mult
-            )
-
-        work = ctx.enter_context(tc.tile_pool(name="work", bufs=2))
 
         s_bank, q_bank, st_r, a_bank, t_bank, p_bank = {}, {}, {}, {}, {}, {}
         gt, so, mv_r, rs_r, ahat, p2t, c0s = {}, {}, {}, {}, {}, {}, {}
@@ -314,28 +261,22 @@ def tile_multilstm_pa_t_kernel(
             t = ST * s + bt
             src = gt[t][:, c * H:(c + 1) * H]
             if c == 3:
-                so[t] = work.tile([P, H], F32, name="so", tag="so", bufs=8)
+                so[t] = cellp[0].tile([P, H], F32, name="so", tag="so", bufs=8)
                 nc.scalar.activation(out=so[t][:], in_=src, func=ACT.Sigmoid)
             else:
                 nc.scalar.activation(out=src, in_=src, func=(ACT.Tanh if c == 2 else ACT.Sigmoid))
 
-        def pair_engine(t):
-            return nc.vector if t >= NT - ST else nc.gpsimd
-
-        def c12(t):
-            if not inside(t):
-                return
+        def c1op(t, eng):
             s, bt = divmod(t, ST)
-            c1s[t] = work.tile([P, H], F32, name="c1", tag="c1", bufs=3)
-            c2s[t] = work.tile([P, H], F32, name="c2", tag="c2")
-            eng = pair_engine(t)
+            c1s[t] = cellp[0].tile([P, H], F32, name="c1", tag="c1", bufs=C1_BUFS)
             eng.tensor_tensor(out=c1s[t][:], in0=gt[t][:, H:2 * H], in1=c0s[s][:, bt, :], op=ALU.mult)
+
+        def c2op(t, eng):
+            c2s[t] = cellp[0].tile([P, H], F32, name="c2", tag="c2", bufs=C2_BUFS)
             eng.tensor_tensor(out=c2s[t][:], in0=gt[t][:, 0:H], in1=gt[t][:, 2 * H:3 * H], op=ALU.mult)
 
-        def csum(t):
-            if not inside(t):
-                return
-            pair_engine(t).tensor_tensor(out=c1s[t][:], in0=c1s[t][:], in1=c2s[t][:], op=ALU.add)
+        def csum(t, eng):
+            eng.tensor_tensor(out=c1s[t][:], in0=c1s[t][:], in1=c2s[t][:], op=ALU.add)
 
         def cstat(t):
             if not inside(t):
@@ -354,7 +295,7 @@ def tile_multilstm_pa_t_kernel(
         def yop(t):
             if not inside(t):
                 return
-            ys[t] = work.tile([P, H], F32, name="y", tag="y")
+            ys[t] = cellp[0].tile([P, H], F32, name="y", tag="y")
             nc.vector.scalar_tensor_tensor(
                 out=ys[t][:], in0=c1s[t][:], scalar=mv_c[t][:, 0:1], in1=cw_bc[:], op0=ALU.subtract, op1=ALU.mult
             )
@@ -362,7 +303,7 @@ def tile_multilstm_pa_t_kernel(
         def cyop(t):
             if not inside(t):
                 return
-            cys[t] = work.tile([P, H], F32, name="cy", tag="cy", bufs=3)
+            cys[t] = cellp[0].tile([P, H], F32, name="cy", tag="cy", bufs=3)
             nc.vector.scalar_tensor_tensor(
                 out=cys[t][:], in0=ys[t][:], scalar=rs_c[t][:, 0:1], in1=cb_bc[:], op0=ALU.mult, op1=ALU.add
             )
@@ -371,46 +312,194 @@ def tile_multilstm_pa_t_kernel(
         def th(t):
             if not inside(t):
                 return
-            tcs[t] = work.tile([P, H], F32, name="tcy", tag="tcy", bufs=3)
+            tcs[t] = cellp[0].tile([P, H], F32, name="tcy", tag="tcy", bufs=3)
             nc.scalar.activation(out=tcs[t][:], in_=cys[t][:], func=ACT.Tanh)
 
-        def hyop(t):
-            if not inside(t):
-                return
-            hy = work.tile([P, H], F32, name="hy", tag="hy", bufs=3)
-            eng = nc.vector if t >= NT - 2 * ST else nc.gpsimd
+        def hyop(t, eng):
+            hy = cellp[0].tile([P, H], F32, name="hy", tag="hy", bufs=4)
             eng.tensor_tensor(out=hy[:], in0=so[t][:], in1=tcs[t][:], op=ALU.mult)
             nc.sync.dma_start(out=hy_v[:, t, :], in_=hy[:])
 
-        with tc.manual_schedule():
-            for n in range(-6, NT + 9):
-                if n % ST == 0 and inside(n):
-                    c0s[n // ST] = work.tile([P, ST, H], BF16, name="c0_sb", tag="c0_sb", bufs=3)
-                    nc.sync.dma_start(out=c0s[n // ST][:], in_=c0_v[:, n:n + ST, :])
-                for i in range(4):
-                    n1, i1 = divmod(4 * n + i + 1, 4)
-                    n2, i2 = divmod(4 * n + i + 2, 4)
-                    ah(n + 2, i)
-                    tb(n1 + 1, i1)
-                    pt(n + 1, i)
-                    am(n2 + 2, i2)
-                    act(n - 1, i)
-                    fill_st(n1 + 5, i1)
-                    rd_st(n + 5, i)
-                    fill_q(n1 + 4, i1)
-                    rd_q(n + 4, i)
-                    p2(n1, i1)
-                    z(n, i)
-                    if i == 0:
-                        c12(n - 4)
-                        cstat(n - 5)
-                    elif i == 1:
-                        cpow(n - 5)
-                        csum(n - 4)
-                        cyop(n - 6)
-                        th(n - 7)
-                    elif i == 2:
-                        yop(n - 5)
-                        hyop(n - 8)
+
+        two_input = {"c1": c1op, "c2": c2op, "csum": csum, "hy": hyop}
+        one_engine = {"cstat": cstat, "cpow": cpow, "y": yop, "cy": cyop, "th": th}
+        plan = CELL_PLAN()
+
+        def slot(n, prep):
+            if n % ST == 0 and inside(n):
+                c0s[n // ST] = work.tile([P, ST, H], BF16, name="c0_sb", tag="c0_sb", bufs=3)
+                nc.sync.dma_start(out=c0s[n // ST][:], in_=c0_v[:, n:n + ST, :])
+            for i in range(4):
+                n1, i1 = divmod(4 * n + i + 1, 4)
+                n2, i2 = divmod(4 * n + i + 2, 4)
+                ah(n + 2, i)
+                tb(n1 + 1, i1)
+                pt(n + 1, i)
+                am(n2 + 2, i2)
+                act(n - 1, i)
+                fill_st(n1 + 5, i1)
+                rd_st(n + 5, i)
+                fill_q(n1 + 4, i1)
+                rd_q(n + 4, i)
+                p2(n1, i1)
+                z(n, i)
+                for name, t, on_vector in plan.get((n, i), []):
+                    if name in two_input:
+                        two_input[name](t, nc.vector if on_vector else nc.gpsimd)
                     else:
-                        aggr(n + 5)
+                        one_engine[name](t)
+                if i == 3:
+                    aggr(n + 5)
+                for job in prep.get((n, i), []):
+                    job()
+
+        with tc.tile_pool(name="pro", bufs=1) as pro, tc.tile_pool(name="stage", bufs=2) as stg:
+            x_sb = pro.tile([P, NT, V], BF16, name="x_sb")
+            w_n = pro.tile([P, 16, V], BF16, name="w_n")
+            vec = pro.tile([P, P], BF16, name="vec")
+            nc.vector.memset(vec[:], 0.0)
+
+            raws = {}
+            groupeds = {}
+            y_bank = {}
+
+            def load_rows(j):
+                if 1 <= j <= 4:
+                    src = whh_v[:, ST * (j - 1):ST * j, :]
+                else:
+                    s = max(j - 4, 0)
+                    src = h0_v[:, ST * s:ST * (s + 1), :]
+                raws[j] = stg.tile([P, ST * H], BF16, name="raw", tag="raw", bufs=RAW_BUFS)
+                nc.sync.dma_start(out=raws[j][:].rearrange("p (t k) -> p t k", t=ST), in_=src)
+
+            def pack_rows(j):
+                words = raws[j][:].bitcast(F32)
+                grouped = stg.tile([P, ST * P * 4], BF16, name="grouped", tag="grouped", bufs=GROUPED_BUFS, align_bytes=64)
+                groupeds[j] = grouped
+                g_words = grouped[:].bitcast(F32).rearrange("p (t c u) -> p t c u", t=ST, u=2)
+                for half in range(2):
+                    bank = psum.tile([P, 2, 2, P], F32, name="tp_w", tag="ss")
+                    for i in range(2):
+                        for u in range(2):
+                            col = (2 * half + i) * (H // 2) + u * P
+                            nc.tensor.transpose(bank[:, i, u, :], words[:, col:col + P], ident_f[:])
+                    nc.scalar.copy(
+                        out=g_words[:, 2 * half:2 * half + 2, :, :], in_=bank[:].rearrange("p t u c -> p t c u")
+                    )
+                if j + RAW_BUFS < 12:
+                    load_rows(j + RAW_BUFS)
+
+            def quant_rows(j):
+                is_w = 1 <= j <= 4
+                first = (j - 1 if is_w else max(j - 4, 0)) * H
+                cols = slice(first, first + H)
+                codes = w_codes[:, cols] if is_w else h_codes[:, cols]
+                scales = w_scales[:, cols] if is_w else h_scales[:, cols]
+                nc.vector.quantize_mx(out=codes.bitcast(FP8X4), scales=scales, in_=groupeds[j][:])
+
+            def vec_t():
+                bank = psum.tile([P, P], BF16, name="tp_v", tag="vs")
+                nc.tensor.transpose(bank[:], vec[:], ident_b[:])
+                nc.vector.tensor_copy(out=v_t[:], in_=bank[:, 0:48])
+                nc.vector.tensor_tensor(out=b_t[:], in0=v_t[:, 16:32], in1=v_t[:, 32:48], op=ALU.add)
+
+            def flip(dst, src, g):
+                bank = psum.tile([P, 4, P], BF16, name="tp_b", tag="ss")
+                for i in range(4):
+                    nc.tensor.transpose(bank[:, i, :], src[:, 4 * g + i, :], ident_b[:])
+                nc.scalar.copy(out=dst[:, 4 * g * P:4 * (g + 1) * P], in_=bank[:].rearrange("p t c -> p (t c)"))
+
+            def gram():
+                g_ps = psum.tile([P, P + 2], F32, name="g_ps", tag="vs")
+                for t in range(16):
+                    nc.tensor.matmul(
+                        g_ps[:, 0:P], lhsT=w_n[:, t, :], rhs=w_n[:, t, :], start=(t == 0), stop=(t == 15)
+                    )
+                for t in range(16):
+                    nc.tensor.matmul(
+                        g_ps[:, P:P + 2], lhsT=w_n[:, t, :], rhs=ones_b[:], start=(t == 0), stop=(t == 15)
+                    )
+                nc.vector.tensor_copy(out=g_hl[:, 0, :], in_=g_ps[:])
+                nc.vector.tensor_tensor(out=g_hl[:, 1, :], in0=g_ps[:], in1=g_hl[:, 0, :], op=ALU.subtract)
+
+            def a_mm(t0):
+                y_ps = psum.tile([P, 2, P + 2], F32, name="y_ps", tag="ss")
+                for i in range(2):
+                    lhs = x_t[:, (t0 + i) * P:(t0 + i + 1) * P]
+                    nc.tensor.matmul(y_ps[:, i, :], lhsT=lhs, rhs=g_hl[:, 0, :], start=True, stop=False)
+                    nc.tensor.matmul(y_ps[:, i, :], lhsT=lhs, rhs=g_hl[:, 1, :], start=False, stop=True)
+                y_bank[t0] = y_ps
+
+            def a_red(t0):
+                y_ps = y_bank[t0]
+                for i in range(2):
+                    junk = pro.tile([P, P], F32, name="junk", tag="junk", bufs=2)
+                    nc.vector.scalar_tensor_tensor(
+                        out=junk[:],
+                        in0=y_ps[:, i, 0:P],
+                        scalar=1.0,
+                        in1=x_sb[:, t0 + i, :],
+                        op0=ALU.mult,
+                        op1=ALU.mult,
+                        accum_out=sumsq_a[:, t0 + i:t0 + i + 1],
+                    )
+                nc.vector.tensor_copy(out=sum_a[:, t0:t0 + 2], in_=y_ps[:, :, P])
+
+            def a_finish(lo, hi):
+                c = slice(lo, hi)
+                nc.vector.tensor_scalar(out=mu_a[:, c], in0=sum_a[:, c], scalar1=1.0 / G, scalar2=None, op0=ALU.mult)
+                nc.vector.tensor_tensor(out=musq_a[:, c], in0=mu_a[:, c], in1=mu_a[:, c], op=ALU.mult)
+                nc.vector.scalar_tensor_tensor(
+                    out=var_a[:, c], in0=sumsq_a[:, c], scalar=1.0 / G, in1=musq_a[:, c], op0=ALU.mult, op1=ALU.subtract
+                )
+                nc.vector.tensor_scalar(
+                    out=ve_a[:, c], in0=var_a[:, c], scalar1=0.0, scalar2=EPS, op0=ALU.max, op1=ALU.add
+                )
+                nc.gpsimd.tensor_tensor(out=rs_a[:, c], in0=ve_a[:, c], in1=mhalf[:, c], op=ALU.pow)
+
+            def a_bias(lo, hi):
+                c = slice(lo, hi)
+                nc.vector.scalar_tensor_tensor(
+                    out=nb_a[:, c], in0=mu_a[:, c], scalar=-1.0, in1=rs_a[:, c], op0=ALU.mult, op1=ALU.mult
+                )
+
+            for j in range(RAW_BUFS):
+                load_rows(j)
+            nc.sync.dma_start(out=wh_bc[:], in_=lnh_w1.partition_broadcast(P))
+            nc.sync.dma_start(out=w_n[:], in_=wih_v)
+            nc.sync.dma_start(out=x_sb[:], in_=x_v)
+            for j in range(5):
+                pack_rows(j)
+                quant_rows(j)
+            nc.sync.dma_start(out=vec[0:16, :], in_=lni_w1.rearrange("(t p) -> t p", p=P))
+            nc.sync.dma_start(out=vec[16:32, :], in_=lni_b1.rearrange("(t p) -> t p", p=P))
+            nc.sync.dma_start(out=vec[32:48, :], in_=lnh_b1.rearrange("(t p) -> t p", p=P))
+            nc.sync.dma_start(out=cw_bc[:], in_=lnc_w1.partition_broadcast(P))
+            nc.sync.dma_start(out=cb_bc[:], in_=lnc_b1.partition_broadcast(P))
+            flip(w_t, w_n, 0)
+            flip(x_t, x_sb, 0)
+            gram()
+            for t0 in (0, 2):
+                a_mm(t0)
+                a_red(t0)
+            a_finish(0, 4)
+            a_bias(0, 4)
+            vec_t()
+            pack_rows(5)
+            quant_rows(5)
+            for g in range(1, 4):
+                flip(w_t, w_n, g)
+            for g in range(1, 8):
+                flip(x_t, x_sb, g)
+                for t0 in (4 * g, 4 * g + 2):
+                    a_mm(t0)
+                    a_red(t0)
+            a_finish(4, NT)
+            a_bias(4, NT)
+            for j in range(6, 12):
+                pack_rows(j)
+                quant_rows(j)
+        cellp.append(ctx.enter_context(tc.tile_pool(name="cellp", bufs=2)))
+        with tc.manual_schedule():
+            for n in range(-6, LAST_SLOT + 1):
+                slot(n, {})

@@ -32,20 +32,23 @@ def CELL_PLAN():
     plan = {}
 
     def put(n, i, name, t, on_vector=False):
+        n, i = n + i // 4, i % 4
         if (n, i) not in plan:
             plan[(n, i)] = []
         plan[(n, i)].append((name, t, on_vector))
 
     for t in range(NT - 2 * ST):
-        put(t + 4, 0, "c1", t)
-        put(t + 4, 0, "c2", t)
+        put(t + 6, 0, "tw", t)
+        put(t + 6, 0, "cyg", t)
         put(t + 5, 0, "cstat", t)
-        put(t + 5, 1, "cpow", t)
-        put(t + 4, 1, "csum", t)
-        put(t + 5, 1, "y", t)
-        put(t + 5, 2, "cy", t)
-        put(t + 6, 2, "hy", t)
-        put(t + 5, 3, "th", t)
+        put(t + 5, 0, "cpow", t)
+        put(t + 4, 0, "c1", t)
+        put(t + 4, 1, "c2", t)
+        put(t + 4, 2, "csum", t)
+        put(t + 5, 2, "nb", t)
+        put(t + 5, 3, "n", t)
+        put(t + 6, 2, "th", t)
+        put(t + 6, 4, "hy", t, True)
     for j, t in enumerate(range(NT - 2 * ST, NT - ST)):
         n = NT - ST + j // 2
         v = j % 2 == 1
@@ -60,10 +63,10 @@ def CELL_PLAN():
         put(n + 2, 2 + v, "hy", t, True)
     for j, t in enumerate(range(NT - ST, NT)):
         m = 4 * (NT - 1) + j
-        put((m - 2) // 4, (m - 2) % 4, "c1", t)
+        put(0, m - 2, "c1", t)
         for d, names in ((1, ("c2", "csum", "cstat")), (2, ("cpow", "y")), (3, ("cy",)), (4, ("th",)), (5, ("hy",))):
             for name in names:
-                put((m + d) // 4, (m + d) % 4, name, t, True)
+                put(0, m + d, name, t, True)
     return plan
 
 
@@ -120,6 +123,7 @@ def tile_multilstm_pa_t_kernel(
         s_bank, q_bank, st_r, a_bank, t_bank, p_bank = {}, {}, {}, {}, {}, {}
         gt, so, mv_r, rs_r, ahat, p2t, c0s = {}, {}, {}, {}, {}, {}, {}
         c1s, c2s, ys, cys, tcs, mv_c, rs_c = {}, {}, {}, {}, {}, {}, {}
+        nb_c = {}
 
         def inside(i):
             return 0 <= i < NT
@@ -295,7 +299,7 @@ def tile_multilstm_pa_t_kernel(
         def yop(t):
             if not inside(t):
                 return
-            ys[t] = cellp[0].tile([P, H], F32, name="y", tag="y")
+            ys[t] = cellp[0].tile([P, H], F32, name="y", tag="y", bufs=3)
             nc.vector.scalar_tensor_tensor(
                 out=ys[t][:], in0=c1s[t][:], scalar=mv_c[t][:, 0:1], in1=cw_bc[:], op0=ALU.subtract, op1=ALU.mult
             )
@@ -307,6 +311,26 @@ def tile_multilstm_pa_t_kernel(
             nc.vector.scalar_tensor_tensor(
                 out=cys[t][:], in0=ys[t][:], scalar=rs_c[t][:, 0:1], in1=cb_bc[:], op0=ALU.mult, op1=ALU.add
             )
+            nc.sync.dma_start(out=cy_v[:, t, :], in_=cys[t][:])
+
+        def nbop(t):
+            nb_c[t] = small.tile([P, 1], F32, name="nb_c", tag="nb_c", bufs=3)
+            nc.vector.scalar_tensor_tensor(
+                out=nb_c[t][:], in0=mv_c[t][:, 0:1], scalar=-1.0, in1=rs_c[t][:], op0=ALU.mult, op1=ALU.mult
+            )
+
+        def nop(t):
+            ys[t] = cellp[0].tile([P, H], F32, name="y", tag="y", bufs=3)
+            nc.scalar.activation(
+                out=ys[t][:], in_=c1s[t][:], func=ACT.Identity, bias=nb_c[t][:, 0:1], scale=rs_c[t][:, 0:1]
+            )
+
+        def twop(t):
+            nc.gpsimd.tensor_tensor(out=ys[t][:], in0=ys[t][:], in1=cw_bc[:], op=ALU.mult)
+
+        def cygop(t):
+            cys[t] = cellp[0].tile([P, H], F32, name="cy", tag="cy", bufs=3)
+            nc.gpsimd.tensor_tensor(out=cys[t][:], in0=ys[t][:], in1=cb_bc[:], op=ALU.add)
             nc.sync.dma_start(out=cy_v[:, t, :], in_=cys[t][:])
 
         def th(t):
@@ -322,7 +346,7 @@ def tile_multilstm_pa_t_kernel(
 
 
         two_input = {"c1": c1op, "c2": c2op, "csum": csum, "hy": hyop}
-        one_engine = {"cstat": cstat, "cpow": cpow, "y": yop, "cy": cyop, "th": th}
+        one_engine = {"cstat": cstat, "cpow": cpow, "y": yop, "cy": cyop, "th": th, "nb": nbop, "n": nop, "tw": twop, "cyg": cygop}
         plan = CELL_PLAN()
 
         def slot(n, prep):

@@ -32,23 +32,24 @@ def CELL_PLAN():
     plan = {}
 
     def put(n, i, name, t, on_vector=False):
-        n, i = n + i // 4, i % 4
         if (n, i) not in plan:
             plan[(n, i)] = []
         plan[(n, i)].append((name, t, on_vector))
 
     for t in range(NT - 2 * ST):
-        put(t + 6, 0, "tw", t)
-        put(t + 6, 0, "cyg", t)
-        put(t + 5, 0, "cstat", t)
-        put(t + 5, 0, "cpow", t)
         put(t + 4, 0, "c1", t)
-        put(t + 4, 1, "c2", t)
-        put(t + 4, 2, "csum", t)
-        put(t + 5, 2, "nb", t)
-        put(t + 5, 3, "n", t)
-        put(t + 6, 2, "th", t)
-        put(t + 6, 4, "hy", t, True)
+        put(t + 4, 0, "c2", t)
+        if t % 2 in (1,):
+            put(t + 4, 3, "cs1", t)
+            put(t + 5, 0, "cs2", t)
+        else:
+            put(t + 5, 0, "cstat", t)
+        put(t + 5, 1, "cpow", t)
+        put(t + 4, 1, "csum", t)
+        put(t + 5, 1, "y", t)
+        put(t + 5, 2, "cy", t)
+        put(t + 6, 2, "hy", t)
+        put(t + 5, 3, "th", t)
     for j, t in enumerate(range(NT - 2 * ST, NT - ST)):
         n = NT - ST + j // 2
         v = j % 2 == 1
@@ -63,10 +64,10 @@ def CELL_PLAN():
         put(n + 2, 2 + v, "hy", t, True)
     for j, t in enumerate(range(NT - ST, NT)):
         m = 4 * (NT - 1) + j
-        put(0, m - 2, "c1", t)
+        put((m - 2) // 4, (m - 2) % 4, "c1", t)
         for d, names in ((1, ("c2", "csum", "cstat")), (2, ("cpow", "y")), (3, ("cy",)), (4, ("th",)), (5, ("hy",))):
             for name in names:
-                put(0, m + d, name, t, True)
+                put((m + d) // 4, (m + d) % 4, name, t, True)
     return plan
 
 
@@ -123,7 +124,7 @@ def tile_multilstm_pa_t_kernel(
         s_bank, q_bank, st_r, a_bank, t_bank, p_bank = {}, {}, {}, {}, {}, {}
         gt, so, mv_r, rs_r, ahat, p2t, c0s = {}, {}, {}, {}, {}, {}, {}
         c1s, c2s, ys, cys, tcs, mv_c, rs_c = {}, {}, {}, {}, {}, {}, {}
-        nb_c = {}
+        nmu_c, var_c = {}, {}
 
         def inside(i):
             return 0 <= i < NT
@@ -291,17 +292,36 @@ def tile_multilstm_pa_t_kernel(
             nc.vector.bn_aggr(out=mv[:], in_=st6[:])
             mv_c[t] = mv
 
+        def cs1(t):
+            junk = small.tile([P, H], BF16, name="junk_c", tag="junk_c")
+            total = small.tile([P, 1], F32, name="sum_c", tag="sum_c")
+            nc.scalar.activation(out=junk[:], in_=c1s[t][:], func=ACT.Identity, accum_out=total[:])
+            nmu_c[t] = small.tile([P, 1], F32, name="nmu_c", tag="nmu_c", bufs=3)
+            nc.scalar.activation(out=nmu_c[t][:], in_=total[:], func=ACT.Identity, scale=-1.0 / H)
+
+        def cs2(t):
+            junk = small.tile([P, H], BF16, name="junk_c", tag="junk_c")
+            ssq = small.tile([P, 1], F32, name="ssq_c", tag="ssq_c")
+            nc.scalar.activation(out=junk[:], in_=c1s[t][:], func=ACT.Square, bias=nmu_c[t][:, 0:1], accum_out=ssq[:])
+            var_c[t] = small.tile([P, 1], F32, name="var_c", tag="var_c", bufs=3)
+            nc.scalar.activation(out=var_c[t][:], in_=ssq[:], func=ACT.Identity, scale=1.0 / H)
+
         def cpow(t):
             if not inside(t):
                 return
-            rs_c[t] = rsqrt_eps(mv_c[t][:, 1:2], "c", 3)
+            rs_c[t] = rsqrt_eps(var_c[t][:, 0:1] if t in var_c else mv_c[t][:, 1:2], "c", 3)
 
         def yop(t):
             if not inside(t):
                 return
-            ys[t] = cellp[0].tile([P, H], F32, name="y", tag="y", bufs=3)
+            ys[t] = cellp[0].tile([P, H], F32, name="y", tag="y")
             nc.vector.scalar_tensor_tensor(
-                out=ys[t][:], in0=c1s[t][:], scalar=mv_c[t][:, 0:1], in1=cw_bc[:], op0=ALU.subtract, op1=ALU.mult
+                out=ys[t][:],
+                in0=c1s[t][:],
+                scalar=(nmu_c[t][:, 0:1] if t in nmu_c else mv_c[t][:, 0:1]),
+                in1=cw_bc[:],
+                op0=(ALU.add if t in nmu_c else ALU.subtract),
+                op1=ALU.mult,
             )
 
         def cyop(t):
@@ -311,26 +331,6 @@ def tile_multilstm_pa_t_kernel(
             nc.vector.scalar_tensor_tensor(
                 out=cys[t][:], in0=ys[t][:], scalar=rs_c[t][:, 0:1], in1=cb_bc[:], op0=ALU.mult, op1=ALU.add
             )
-            nc.sync.dma_start(out=cy_v[:, t, :], in_=cys[t][:])
-
-        def nbop(t):
-            nb_c[t] = small.tile([P, 1], F32, name="nb_c", tag="nb_c", bufs=3)
-            nc.vector.scalar_tensor_tensor(
-                out=nb_c[t][:], in0=mv_c[t][:, 0:1], scalar=-1.0, in1=rs_c[t][:], op0=ALU.mult, op1=ALU.mult
-            )
-
-        def nop(t):
-            ys[t] = cellp[0].tile([P, H], F32, name="y", tag="y", bufs=3)
-            nc.scalar.activation(
-                out=ys[t][:], in_=c1s[t][:], func=ACT.Identity, bias=nb_c[t][:, 0:1], scale=rs_c[t][:, 0:1]
-            )
-
-        def twop(t):
-            nc.gpsimd.tensor_tensor(out=ys[t][:], in0=ys[t][:], in1=cw_bc[:], op=ALU.mult)
-
-        def cygop(t):
-            cys[t] = cellp[0].tile([P, H], F32, name="cy", tag="cy", bufs=3)
-            nc.gpsimd.tensor_tensor(out=cys[t][:], in0=ys[t][:], in1=cb_bc[:], op=ALU.add)
             nc.sync.dma_start(out=cy_v[:, t, :], in_=cys[t][:])
 
         def th(t):
@@ -346,7 +346,7 @@ def tile_multilstm_pa_t_kernel(
 
 
         two_input = {"c1": c1op, "c2": c2op, "csum": csum, "hy": hyop}
-        one_engine = {"cstat": cstat, "cpow": cpow, "y": yop, "cy": cyop, "th": th, "nb": nbop, "n": nop, "tw": twop, "cyg": cygop}
+        one_engine = {"cstat": cstat, "cpow": cpow, "y": yop, "cy": cyop, "th": th, "cs1": cs1, "cs2": cs2}
         plan = CELL_PLAN()
 
         def slot(n, prep):
@@ -487,19 +487,31 @@ def tile_multilstm_pa_t_kernel(
                     out=nb_a[:, c], in0=mu_a[:, c], scalar=-1.0, in1=rs_a[:, c], op0=ALU.mult, op1=ALU.mult
                 )
 
+            rows_b = pro.tile([P, G + 2 * H], BF16, name="rows_b")
+            nc.vector.memset(rows_b[:], 0.0)
+            ones_sq = pro.tile([P, P], BF16, name="ones_sq")
+            nc.vector.memset(ones_sq[:], 1.0)
+
+            def spread(dst, first):
+                bank = psum.tile([P, H], F32, name="b_ps", tag="ss")
+                nc.tensor.matmul(bank[:], lhsT=ones_sq[:], rhs=rows_b[:, first:first + H], start=True, stop=True)
+                nc.scalar.copy(out=dst, in_=bank[:])
+
             for j in range(RAW_BUFS):
                 load_rows(j)
-            nc.sync.dma_start(out=wh_bc[:], in_=lnh_w1.partition_broadcast(P))
+            nc.sync.dma_start(out=rows_b[0:1, 0:G], in_=lnh_w1.rearrange("(o g) -> o g", o=1))
+            nc.sync.dma_start(out=rows_b[0:1, G:G + H], in_=lnc_w1.rearrange("(o g) -> o g", o=1))
+            nc.sync.dma_start(out=rows_b[0:1, G + H:G + 2 * H], in_=lnc_b1.rearrange("(o g) -> o g", o=1))
             nc.sync.dma_start(out=w_n[:], in_=wih_v)
             nc.sync.dma_start(out=x_sb[:], in_=x_v)
             for j in range(5):
                 pack_rows(j)
                 quant_rows(j)
+            for c in range(4):
+                spread(wh_bc[:, c * H:(c + 1) * H], c * H)
             nc.sync.dma_start(out=vec[0:16, :], in_=lni_w1.rearrange("(t p) -> t p", p=P))
             nc.sync.dma_start(out=vec[16:32, :], in_=lni_b1.rearrange("(t p) -> t p", p=P))
             nc.sync.dma_start(out=vec[32:48, :], in_=lnh_b1.rearrange("(t p) -> t p", p=P))
-            nc.sync.dma_start(out=cw_bc[:], in_=lnc_w1.partition_broadcast(P))
-            nc.sync.dma_start(out=cb_bc[:], in_=lnc_b1.partition_broadcast(P))
             flip(w_t, w_n, 0)
             flip(x_t, x_sb, 0)
             gram()
@@ -520,6 +532,8 @@ def tile_multilstm_pa_t_kernel(
                     a_red(t0)
             a_finish(4, NT)
             a_bias(4, NT)
+            spread(cw_bc[:], G)
+            spread(cb_bc[:], G + H)
             for j in range(6, 12):
                 pack_rows(j)
                 quant_rows(j)

from contextlib import ExitStack

import concourse.mybir as mybir
from concourse.masks import make_identity

F32 = mybir.dt.float32
BF16 = mybir.dt.bfloat16
U32 = mybir.dt.uint32
U8 = mybir.dt.uint8
FP8X4 = mybir.dt.float8_e4m3fn_x4
ALU = mybir.AluOpType
ACT = mybir.ActivationFunctionType
AX = mybir.AxisListType

P = 128
B, V, H = 4096, 128, 512
G = 4 * H
NT = B // P
ST = 4
EPS = 1e-5
FLOPS = 2 * B * G * (H + V)

RAW_BUFS = 5
GROUPED_BUFS = 5

C1_BUFS = 6
C2_BUFS = 3
LAST_SLOT = NT + 1


def CELL_PLAN():
    plan = {}

    def put(n, i, name, t, on_vector=False):
        if (n, i) not in plan:
            plan[(n, i)] = []
        plan[(n, i)].append((name, t, on_vector))

    for t in range(NT - 2 * ST):
        put(t + 4, 0, "c1", t)
        put(t + 4, 0, "c2", t)
        if t % 2 in (1,):
            put(t + 4, 3, "cs1", t)
            put(t + 5, 0, "cs2", t)
        else:
            put(t + 5, 0, "cstat", t)
        put(t + 5, 1, "cpow", t)
        put(t + 4, 1, "csum", t)
        put(t + 5, 1, "y", t)
        put(t + 5, 2, "cy", t)
        put(t + 6, 2, "hy", t)
        put(t + 5, 3, "th", t)
    for j, t in enumerate(range(NT - 2 * ST, NT - ST)):
        n = NT - ST + j // 2
        v = j % 2 == 1
        put(n, 0 + v, "c1", t, v)
        put(n, 0 + v, "c2", t, v)
        put(n, 1 + v, "csum", t, v)
        put(n + 1, 0 + v, "cstat", t)
        put(n + 1, 1 + v, "cpow", t)
        put(n + 1, 1 + v, "y", t)
        put(n + 1, 2 + v, "cy", t)
        put(n + 2, 0 + v, "th", t)
        put(n + 2, 2 + v, "hy", t, True)
    for j, t in enumerate(range(NT - ST, NT)):
        m = 4 * (NT - 1) + j
        put((m - 2) // 4, (m - 2) % 4, "c1", t)
        for d, names in ((1, ("c2", "csum", "cstat")), (2, ("cpow", "y")), (3, ("cy",)), (4, ("th",)), (5, ("hy",))):
            for name in names:
                put((m + d) // 4, (m + d) % 4, name, t, True)
    return plan


def tile_multilstm_pa_t_kernel(
    tc, x, h0, c0, w_ih1, w_hh1, lni_w1, lni_b1, lnh_w1, lnh_b1, lnc_w1, lnc_b1, out_0, out_1
):
    nc = tc.nc
    x_v = x.rearrange("(p t) v -> p t v", t=NT)
    h0_v = h0.rearrange("(p t) k -> p t k", t=NT)
    c0_v = c0.rearrange("(p t) k -> p t k", t=NT)
    hy_v = out_0.rearrange("(p t) k -> p t k", t=NT)
    cy_v = out_1.rearrange("(p t) k -> p t k", t=NT)
    whh_v = w_hh1.rearrange("(t p) k -> p t k", p=P)
    wih_v = w_ih1.rearrange("(t p) v -> p t v", p=P)

    with ExitStack() as ctx:
        const = ctx.enter_context(tc.tile_pool(name="const", bufs=1))
        small = ctx.enter_context(tc.tile_pool(name="small", bufs=2))
        gates = ctx.enter_context(tc.tile_pool(name="gates", bufs=9))
        work = ctx.enter_context(tc.tile_pool(name="work", bufs=2))
        psum = ctx.enter_context(tc.psum_pool(name="psum", bufs=4))
        cellp = []

        ident_f = const.tile([P, P], F32, name="ident_f")
        make_identity(nc, ident_f[:])
        ident_b = const.tile([P, P], BF16, name="ident_b")
        make_identity(nc, ident_b[:])
        mhalf = const.tile([P, NT], F32, name="mhalf")
        nc.vector.memset(mhalf[:], -0.5)
        ones_b = const.tile([P, 2], BF16, name="ones_b")
        nc.vector.memset(ones_b[:], 1.0)

        w_codes = const.tile([P, G], U32, name="w_codes", align_bytes=64)
        w_scales = const.tile([P, G], U8, name="w_scales", align_bytes=64)
        h_codes = const.tile([P, B], U32, name="h_codes", align_bytes=64)
        h_scales = const.tile([P, B], U8, name="h_scales", align_bytes=64)
        x_t = const.tile([P, B], BF16, name="x_t")
        w_t = const.tile([P, G], BF16, name="w_t")
        wh_bc = const.tile([P, G], BF16, name="wh_bc")
        cw_bc = const.tile([P, H], BF16, name="cw_bc")
        cb_bc = const.tile([P, H], BF16, name="cb_bc")
        g_hl = const.tile([P, 2, P + 2], BF16, name="g_hl")
        v_t = const.tile([P, 48], F32, name="v_t")
        b_t = const.tile([P, 16], F32, name="b_t")
        sum_a = const.tile([P, NT], F32, name="sum_a")
        sumsq_a = const.tile([P, NT], F32, name="sumsq_a")
        mu_a = const.tile([P, NT], F32, name="mu_a")
        musq_a = const.tile([P, NT], F32, name="musq_a")
        var_a = const.tile([P, NT], F32, name="var_a")
        ve_a = const.tile([P, NT], F32, name="ve_a")
        rs_a = const.tile([P, NT], F32, name="rs_a")
        nb_a = const.tile([P, NT], F32, name="nb_a")

        s_bank, q_bank, st_r, a_bank, t_bank, p_bank = {}, {}, {}, {}, {}, {}
        gt, so, mv_r, rs_r, ahat, p2t, c0s = {}, {}, {}, {}, {}, {}, {}
        c1s, c2s, ys, cys, tcs, mv_c, rs_c = {}, {}, {}, {}, {}, {}, {}
        nmu_c, var_c = {}, {}

        def inside(i):
            return 0 <= i < NT

        def rsqrt_eps(var, tag, bufs):
            ve = small.tile([P, 1], F32, name="ve_" + tag, tag="ve_" + tag)
            nc.gpsimd.tensor_scalar(out=ve[:], in0=var, scalar1=EPS, scalar2=1.0, op0=ALU.add, op1=ALU.mult)
            rs = small.tile([P, 1], F32, name="rs_" + tag, tag="rs_" + tag, bufs=bufs)
            nc.gpsimd.tensor_tensor(out=rs[:], in0=ve[:], in1=mhalf[:, 0:1], op=ALU.pow)
            return rs

        def r_pass(t, c):
            rows = slice(t * P, (t + 1) * P)
            cols = slice(c * H, (c + 1) * H)
            bank = psum.tile([P, H], F32, name="r_ps", tag="vs", bufs=4)
            nc.tensor.matmul_mx(
                out=bank[:],
                lhsT=h_codes[:, rows].bitcast(FP8X4),
                lhsT_scale=h_scales[:, rows],
                rhs=w_codes[:, cols].bitcast(FP8X4),
                rhs_scale=w_scales[:, cols],
                start=True,
                stop=True,
            )
            return bank

        def fill_st(t, c):
            if inside(t):
                s_bank[(t, c)] = r_pass(t, c)

        def fill_q(t, c):
            if inside(t):
                q_bank[(t, c)] = r_pass(t, c)

        def rd_st(t, c):
            if not inside(t):
                return
            if c == 0:
                st_r[t] = small.tile([P, 4, 6], F32, name="st_r", tag="st_r")
            nc.vector.bn_stats(out=st_r[t][:, c, :], in_=s_bank[(t, c)][:])

        def aggr(t):
            if not inside(t):
                return
            mv = small.tile([P, 2], F32, name="mv_r", tag="mv_r", bufs=3)
            nc.vector.bn_aggr(out=mv[:], in_=st_r[t][:].rearrange("p c s -> p (c s)"))
            mv_r[t] = mv
            rs_r[t] = rsqrt_eps(mv[:, 1:2], "r", 11)

        def rd_q(t, c):
            if not inside(t):
                return
            if c == 0:
                gt[t] = gates.tile([P, G], F32, name="gate", tag="gate")
            cols = slice(c * H, (c + 1) * H)
            nc.vector.scalar_tensor_tensor(
                out=gt[t][:, cols],
                in0=q_bank[(t, c)][:],
                scalar=mv_r[t][:, 0:1],
                in1=wh_bc[:, cols],
                op0=ALU.subtract,
                op1=ALU.mult,
            )

        def am(k, bt):
            if not inside(k):
                return
            s, c = divmod(k, 4)
            t = ST * s + bt
            bank = psum.tile([P, H], F32, name="a_ps", tag="ss", bufs=4)
            nc.tensor.matmul(
                bank[:], lhsT=x_t[:, t * P:(t + 1) * P], rhs=w_t[:, c * H:(c + 1) * H], start=True, stop=True
            )
            a_bank[(k, bt)] = bank

        def ah(k, bt):
            if not inside(k):
                return
            t = ST * (k // 4) + bt
            if bt == 0:
                ahat[k] = work.tile([P, ST, H], F32, name="ahat", tag="ahat")
            nc.scalar.activation(
                out=ahat[k][:, bt, :],
                in_=a_bank[(k, bt)][:],
                func=ACT.Identity,
                bias=nb_a[:, t:t + 1],
                scale=rs_a[:, t:t + 1],
            )

        def tb(k, jb):
            if not inside(k):
                return
            bank = psum.tile([P, ST, P], F32, name="t_ps", tag="ss", bufs=4)
            for bt in range(ST):
                nc.tensor.transpose(bank[:, bt, :], ahat[k][:, bt, jb * P:(jb + 1) * P], ident_f[:])
            t_bank[(k, jb)] = bank

        def pt(k, jb):
            if not inside(k):
                return
            if jb == 0:
                p2t[k] = work.tile([P, 4, ST * P], F32, name="p2t", tag="p2t")
            col = 4 * (k % 4) + jb
            nc.scalar.activation(
                out=p2t[k][:, jb, :],
                in_=t_bank[(k, jb)][:].rearrange("p t b -> p (t b)"),
                func=ACT.Identity,
                bias=b_t[:, col:col + 1],
                scale=v_t[:, col:col + 1],
            )

        def p2(k, bt):
            if not inside(k):
                return
            bank = psum.tile([P, 4, P], F32, name="p_ps", tag="vs", bufs=4)
            for jb in range(4):
                nc.tensor.transpose(bank[:, jb, :], p2t[k][:, jb, bt * P:(bt + 1) * P], ident_f[:])
            p_bank[(k, bt)] = bank

        def z(k, bt):
            if not inside(k):
                return
            s, c = divmod(k, 4)
            t = ST * s + bt
            dst = gt[t][:, c * H:(c + 1) * H]
            nc.vector.scalar_tensor_tensor(
                out=dst,
                in0=dst,
                scalar=rs_r[t][:, 0:1],
                in1=p_bank[(k, bt)][:].rearrange("p j c -> p (j c)"),
                op0=ALU.mult,
                op1=ALU.add,
            )

        def act(k, bt):
            if not inside(k):
                return
            s, c = divmod(k, 4)
            t = ST * s + bt
            src = gt[t][:, c * H:(c + 1) * H]
            if c == 3:
                so[t] = cellp[0].tile([P, H], F32, name="so", tag="so", bufs=8)
                nc.scalar.activation(out=so[t][:], in_=src, func=ACT.Sigmoid)
            else:
                nc.scalar.activation(out=src, in_=src, func=(ACT.Tanh if c == 2 else ACT.Sigmoid))

        def c1op(t, eng):
            s, bt = divmod(t, ST)
            c1s[t] = cellp[0].tile([P, H], F32, name="c1", tag="c1", bufs=C1_BUFS)
            eng.tensor_tensor(out=c1s[t][:], in0=gt[t][:, H:2 * H], in1=c0s[s][:, bt, :], op=ALU.mult)

        def c2op(t, eng):
            c2s[t] = cellp[0].tile([P, H], F32, name="c2", tag="c2", bufs=C2_BUFS)
            eng.tensor_tensor(out=c2s[t][:], in0=gt[t][:, 0:H], in1=gt[t][:, 2 * H:3 * H], op=ALU.mult)

        def csum(t, eng):
            eng.tensor_tensor(out=c1s[t][:], in0=c1s[t][:], in1=c2s[t][:], op=ALU.add)

        def cstat(t):
            if not inside(t):
                return
            st6 = small.tile([P, 6], F32, name="st_c", tag="st_c")
            nc.vector.bn_stats(out=st6[:], in_=c1s[t][:])
            mv = small.tile([P, 2], F32, name="mv_c", tag="mv_c", bufs=3)
            nc.vector.bn_aggr(out=mv[:], in_=st6[:])
            mv_c[t] = mv

        def cs1(t):
            junk = small.tile([P, H], BF16, name="junk_c", tag="junk_c")
            total = small.tile([P, 1], F32, name="sum_c", tag="sum_c")
            nc.scalar.activation(out=junk[:], in_=c1s[t][:], func=ACT.Identity, accum_out=total[:])
            nmu_c[t] = small.tile([P, 1], F32, name="nmu_c", tag="nmu_c", bufs=3)
            nc.scalar.activation(out=nmu_c[t][:], in_=total[:], func=ACT.Identity, scale=-1.0 / H)

        def cs2(t):
            junk = small.tile([P, H], BF16, name="junk_c", tag="junk_c")
            ssq = small.tile([P, 1], F32, name="ssq_c", tag="ssq_c")
            nc.scalar.activation(out=junk[:], in_=c1s[t][:], func=ACT.Square, bias=nmu_c[t][:, 0:1], accum_out=ssq[:])
            var_c[t] = small.tile([P, 1], F32, name="var_c", tag="var_c", bufs=3)
            nc.scalar.activation(out=var_c[t][:], in_=ssq[:], func=ACT.Identity, scale=1.0 / H)

        def cpow(t):
            if not inside(t):
                return
            rs_c[t] = rsqrt_eps(var_c[t][:, 0:1] if t in var_c else mv_c[t][:, 1:2], "c", 3)

        def yop(t):
            if not inside(t):
                return
            ys[t] = cellp[0].tile([P, H], F32, name="y", tag="y")
            nc.vector.scalar_tensor_tensor(
                out=ys[t][:],
                in0=c1s[t][:],
                scalar=(nmu_c[t][:, 0:1] if t in nmu_c else mv_c[t][:, 0:1]),
                in1=cw_bc[:],
                op0=(ALU.add if t in nmu_c else ALU.subtract),
                op1=ALU.mult,
            )

        def cyop(t):
            if not inside(t):
                return
            cys[t] = cellp[0].tile([P, H], F32, name="cy", tag="cy", bufs=3)
            nc.vector.scalar_tensor_tensor(
                out=cys[t][:], in0=ys[t][:], scalar=rs_c[t][:, 0:1], in1=cb_bc[:], op0=ALU.mult, op1=ALU.add
            )
            nc.sync.dma_start(out=cy_v[:, t, :], in_=cys[t][:])

        def th(t):
            if not inside(t):
                return
            tcs[t] = cellp[0].tile([P, H], F32, name="tcy", tag="tcy", bufs=3)
            nc.scalar.activation(out=tcs[t][:], in_=cys[t][:], func=ACT.Tanh)

        def hyop(t, eng):
            hy = cellp[0].tile([P, H], F32, name="hy", tag="hy", bufs=4)
            eng.tensor_tensor(out=hy[:], in0=so[t][:], in1=tcs[t][:], op=ALU.mult)
            nc.sync.dma_start(out=hy_v[:, t, :], in_=hy[:])


        two_input = {"c1": c1op, "c2": c2op, "csum": csum, "hy": hyop}
        one_engine = {"cstat": cstat, "cpow": cpow, "y": yop, "cy": cyop, "th": th, "cs1": cs1, "cs2": cs2}
        plan = CELL_PLAN()

        def slot(n, prep):
            if n % ST == 0 and inside(n):
                c0s[n // ST] = work.tile([P, ST, H], BF16, name="c0_sb", tag="c0_sb", bufs=3)
                nc.sync.dma_start(out=c0s[n // ST][:], in_=c0_v[:, n:n + ST, :])
            for i in range(4):
                n1, i1 = divmod(4 * n + i + 1, 4)
                n2, i2 = divmod(4 * n + i + 2, 4)
                ah(n + 2, i)
                tb(n1 + 1, i1)
                pt(n + 1, i)
                am(n2 + 2, i2)
                act(n - 1, i)
                fill_st(n1 + 5, i1)
                rd_st(n + 5, i)
                fill_q(n1 + 4, i1)
                rd_q(n + 4, i)
                p2(n1, i1)
                z(n, i)
                for name, t, on_vector in plan.get((n, i), []):
                    if name in two_input:
                        two_input[name](t, nc.vector if on_vector else nc.gpsimd)
                    else:
                        one_engine[name](t)
                if i == 3:
                    aggr(n + 5)
                for job in prep.get((n, i), []):
                    job()

        with tc.tile_pool(name="pro", bufs=1) as pro, tc.tile_pool(name="stage", bufs=2) as stg:
            x_sb = pro.tile([P, NT, V], BF16, name="x_sb")
            w_n = pro.tile([P, 16, V], BF16, name="w_n")
            vec = pro.tile([P, P], BF16, name="vec")
            nc.vector.memset(vec[:], 0.0)

            raws = {}
            groupeds = {}
            y_bank = {}

            def load_rows(j):
                if 1 <= j <= 4:
                    src = whh_v[:, ST * (j - 1):ST * j, :]
                else:
                    s = max(j - 4, 0)
                    src = h0_v[:, ST * s:ST * (s + 1), :]
                raws[j] = stg.tile([P, ST * H], BF16, name="raw", tag="raw", bufs=RAW_BUFS)
                nc.sync.dma_start(out=raws[j][:].rearrange("p (t k) -> p t k", t=ST), in_=src)

            def pack_rows(j):
                words = raws[j][:].bitcast(F32)
                grouped = stg.tile([P, ST * P * 4], BF16, name="grouped", tag="grouped", bufs=GROUPED_BUFS, align_bytes=64)
                groupeds[j] = grouped
                g_words = grouped[:].bitcast(F32).rearrange("p (t c u) -> p t c u", t=ST, u=2)
                for half in range(2):
                    bank = psum.tile([P, 2, 2, P], F32, name="tp_w", tag="ss")
                    for i in range(2):
                        for u in range(2):
                            col = (2 * half + i) * (H // 2) + u * P
                            nc.tensor.transpose(bank[:, i, u, :], words[:, col:col + P], ident_f[:])
                    nc.scalar.copy(
                        out=g_words[:, 2 * half:2 * half + 2, :, :], in_=bank[:].rearrange("p t u c -> p t c u")
                    )
                if j + RAW_BUFS < 12:
                    load_rows(j + RAW_BUFS)

            def quant_rows(j):
                is_w = 1 <= j <= 4
                first = (j - 1 if is_w else max(j - 4, 0)) * H
                cols = slice(first, first + H)
                codes = w_codes[:, cols] if is_w else h_codes[:, cols]
                scales = w_scales[:, cols] if is_w else h_scales[:, cols]
                nc.vector.quantize_mx(out=codes.bitcast(FP8X4), scales=scales, in_=groupeds[j][:])

            def vec_t():
                bank = psum.tile([P, P], BF16, name="tp_v", tag="vs")
                nc.tensor.transpose(bank[:], vec[:], ident_b[:])
                nc.vector.tensor_copy(out=v_t[:], in_=bank[:, 0:48])
                nc.vector.tensor_tensor(out=b_t[:], in0=v_t[:, 16:32], in1=v_t[:, 32:48], op=ALU.add)

            def flip(dst, src, g):
                bank = psum.tile([P, 4, P], BF16, name="tp_b", tag="ss")
                for i in range(4):
                    nc.tensor.transpose(bank[:, i, :], src[:, 4 * g + i, :], ident_b[:])
                nc.scalar.copy(out=dst[:, 4 * g * P:4 * (g + 1) * P], in_=bank[:].rearrange("p t c -> p (t c)"))

            def gram():
                g_ps = psum.tile([P, P + 2], F32, name="g_ps", tag="vs")
                for t in range(16):
                    nc.tensor.matmul(
                        g_ps[:, 0:P], lhsT=w_n[:, t, :], rhs=w_n[:, t, :], start=(t == 0), stop=(t == 15)
                    )
                for t in range(16):
                    nc.tensor.matmul(
                        g_ps[:, P:P + 2], lhsT=w_n[:, t, :], rhs=ones_b[:], start=(t == 0), stop=(t == 15)
                    )
                nc.vector.tensor_copy(out=g_hl[:, 0, :], in_=g_ps[:])
                nc.vector.tensor_tensor(out=g_hl[:, 1, :], in0=g_ps[:], in1=g_hl[:, 0, :], op=ALU.subtract)

            def a_mm(t0):
                y_ps = psum.tile([P, 2, P + 2], F32, name="y_ps", tag="ss")
                for i in range(2):
                    lhs = x_t[:, (t0 + i) * P:(t0 + i + 1) * P]
                    nc.tensor.matmul(y_ps[:, i, :], lhsT=lhs, rhs=g_hl[:, 0, :], start=True, stop=False)
                    nc.tensor.matmul(y_ps[:, i, :], lhsT=lhs, rhs=g_hl[:, 1, :], start=False, stop=True)
                y_bank[t0] = y_ps

            def a_red(t0):
                y_ps = y_bank[t0]
                for i in range(2):
                    junk = pro.tile([P, P], F32, name="junk", tag="junk", bufs=2)
                    nc.vector.scalar_tensor_tensor(
                        out=junk[:],
                        in0=y_ps[:, i, 0:P],
                        scalar=1.0,
                        in1=x_sb[:, t0 + i, :],
                        op0=ALU.mult,
                        op1=ALU.mult,
                        accum_out=sumsq_a[:, t0 + i:t0 + i + 1],
                    )
                nc.vector.tensor_copy(out=sum_a[:, t0:t0 + 2], in_=y_ps[:, :, P])

            def a_finish(lo, hi):
                c = slice(lo, hi)
                nc.vector.tensor_scalar(out=mu_a[:, c], in0=sum_a[:, c], scalar1=1.0 / G, scalar2=None, op0=ALU.mult)
                nc.vector.tensor_tensor(out=musq_a[:, c], in0=mu_a[:, c], in1=mu_a[:, c], op=ALU.mult)
                nc.vector.scalar_tensor_tensor(
                    out=var_a[:, c], in0=sumsq_a[:, c], scalar=1.0 / G, in1=musq_a[:, c], op0=ALU.mult, op1=ALU.subtract
                )
                nc.vector.tensor_scalar(
                    out=ve_a[:, c], in0=var_a[:, c], scalar1=0.0, scalar2=EPS, op0=ALU.max, op1=ALU.add
                )
                nc.gpsimd.tensor_tensor(out=rs_a[:, c], in0=ve_a[:, c], in1=mhalf[:, c], op=ALU.pow)

            def a_bias(lo, hi):
                c = slice(lo, hi)
                nc.vector.scalar_tensor_tensor(
                    out=nb_a[:, c], in0=mu_a[:, c], scalar=-1.0, in1=rs_a[:, c], op0=ALU.mult, op1=ALU.mult
                )

            rows_b = pro.tile([P, G + 2 * H], BF16, name="rows_b")
            nc.vector.memset(rows_b[:], 0.0)
            ones_sq = pro.tile([P, P], BF16, name="ones_sq")
            nc.vector.memset(ones_sq[:], 1.0)

            def spread(dst, first):
                bank = psum.tile([P, H], F32, name="b_ps", tag="ss")
                nc.tensor.matmul(bank[:], lhsT=ones_sq[:], rhs=rows_b[:, first:first + H], start=True, stop=True)
                nc.scalar.copy(out=dst, in_=bank[:])

            for j in range(RAW_BUFS):
                load_rows(j)
            nc.sync.dma_start(out=rows_b[0:1, 0:G], in_=lnh_w1.rearrange("(o g) -> o g", o=1))
            nc.sync.dma_start(out=rows_b[0:1, G:G + H], in_=lnc_w1.rearrange("(o g) -> o g", o=1))
            nc.sync.dma_start(out=rows_b[0:1, G + H:G + 2 * H], in_=lnc_b1.rearrange("(o g) -> o g", o=1))
            nc.sync.dma_start(out=w_n[:], in_=wih_v)
            nc.sync.dma_start(out=x_sb[:], in_=x_v)
            for j in range(5):
                pack_rows(j)
                quant_rows(j)
            for c in range(4):
                spread(wh_bc[:, c * H:(c + 1) * H], c * H)
            nc.sync.dma_start(out=vec[0:16, :], in_=lni_w1.rearrange("(t p) -> t p", p=P))
            nc.sync.dma_start(out=vec[16:32, :], in_=lni_b1.rearrange("(t p) -> t p", p=P))
            nc.sync.dma_start(out=vec[32:48, :], in_=lnh_b1.rearrange("(t p) -> t p", p=P))
            flip(w_t, w_n, 0)
            flip(x_t, x_sb, 0)
            gram()
            for t0 in (0, 2):
                a_mm(t0)
                a_red(t0)
            a_finish(0, 4)
            a_bias(0, 4)
            vec_t()
            pack_rows(5)
            quant_rows(5)
            for g in range(1, 4):
                flip(w_t, w_n, g)
            for g in range(1, 8):
                flip(x_t, x_sb, g)
                for t0 in (4 * g, 4 * g + 2):
                    a_mm(t0)
                    a_red(t0)
            a_finish(4, NT)
            a_bias(4, NT)
            spread(cw_bc[:], G)
            spread(cb_bc[:], G + H)
            for j in range(6, 12):
                pack_rows(j)
                quant_rows(j)
        cellp.append(ctx.enter_context(tc.tile_pool(name="cellp", bufs=2)))
        with tc.manual_schedule():
            for n in range(-6, LAST_SLOT + 1):
                slot(n, {})
